import numpy as np
import ml_dtypes


def mxq(x, axis, fmt="e4m3"):
    dtype, down = {"e4m3": (ml_dtypes.float8_e4m3fn, 7), "e5m2": (ml_dtypes.float8_e5m2, 14)}[fmt]
    v = np.moveaxis(np.asarray(x, np.float32).astype(ml_dtypes.bfloat16).astype(np.float64), axis, -1)
    blocks = v.reshape(v.shape[:-1] + (-1, 32))
    amax = np.abs(blocks).max(-1, keepdims=True)
    byte = np.maximum(np.where(amax > 0, np.frexp(amax)[1] - 1 + 127, 0) - down, 1)
    scale = np.exp2(byte - 127.0)
    codes = (blocks / scale).astype(np.float32).astype(dtype).astype(np.float64)
    return np.moveaxis((codes * scale).reshape(v.shape), -1, axis)


WIDE = False


def mx_kscale(k):
    if not WIDE:
        return np.ones(k)
    levels = np.array([10, -10, 5, -5, 0])
    a = np.random.permutation(np.resize(levels, k // 512 * 4)).reshape(k // 512, 4)
    idx = np.arange(k)
    return np.exp2(a[idx // 512, idx % 128 // 32])


BF16 = ml_dtypes.bfloat16


def bf(x):
    return np.asarray(x, np.float32).astype(BF16)


def f64(x):
    return np.asarray(x).astype(np.float64)


B, T, L, D, K = 1, 128, 64, 512, 128
AG = 0.145 * np.sqrt(T)
EPS = 1e-5


def sigmoid(v):
    return 1.0 / (1.0 + np.exp(-v))


def layer_norm(x, g, b):
    m = x.mean(-1, keepdims=True)
    v = ((x - m) ** 2).mean(-1, keepdims=True)
    return (x - m) / np.sqrt(v + EPS) * g + b


def setup_inputs():
    s = mx_kscale(D)
    return {"agg": bf(np.random.standard_normal((B, K, D)) * AG * s),
            "M_old": bf(np.random.standard_normal((B, K, D))),
            "W_ih": bf(np.random.standard_normal((3 * D, D)) / (AG * np.sqrt(D)) / s),
            "W_hh": bf(np.random.standard_normal((3 * D, D)) / np.sqrt(D)),
            "b_ih": bf(np.random.standard_normal(3 * D) * 0.3),
            "b_hh": bf(np.random.standard_normal(3 * D) * 0.3),
            "g_mem": bf(1.0 + 0.1 * np.random.standard_normal(D)),
            "b_mem": bf(0.1 * np.random.standard_normal(D)),
            "Wk": bf(np.random.standard_normal((D, D)) / np.sqrt(D)),
            "Wv": bf(np.random.standard_normal((D, D)) / np.sqrt(D))}


def reference(agg, M_old, W_ih, W_hh, b_ih, b_hh, g_mem, b_mem, Wk, Wv):
    m = f64(M_old)
    gi = (mxq(f64(agg), 2, "e4m3") @ mxq(f64(W_ih), 1, "e4m3").T) + f64(b_ih)
    gh = (mxq(m, 2, "e4m3") @ mxq(f64(W_hh), 1, "e4m3").T) + f64(b_hh)
    gi_r, gi_z, gi_n = np.split(gi, 3, axis=-1)
    gh_r, gh_z, gh_n = np.split(gh, 3, axis=-1)
    r = sigmoid(gi_r + gh_r)
    z = sigmoid(gi_z + gh_z)
    n = np.tanh(gi_n + r * gh_n)
    h_new = (1.0 - z) * n + z * m
    m_new = layer_norm(h_new, f64(g_mem), f64(b_mem))
    mq = mxq(m_new, 2, "e4m3")
    kt = mq @ mxq(f64(Wk), 1, "e4m3").T
    v = mq @ mxq(f64(Wv), 1, "e4m3").T
    return kt, v

@@ -1,0 +1,266 @@
+from contextlib import ExitStack
+
+import concourse.mybir as mybir
+from concourse.masks import make_identity
+
+BF16 = mybir.dt.bfloat16
+F32 = mybir.dt.float32
+U32 = mybir.dt.uint32
+U8 = mybir.dt.uint8
+FP8X4 = mybir.dt.float8_e4m3fn_x4
+ACT = mybir.ActivationFunctionType
+ALU = mybir.AluOpType
+
+P = 128
+D = 512
+PACK = 4
+CHUNKS = D // P
+WORDS = D // 2
+EPS = 1e-5
+
+FLOPS = 2 * P * D * (2 * 3 * D + 2 * D)
+
+
+def tile_instrumentspecificslotmemory_pb_s_kernel(
+    tc, agg, M_old, W_ih, W_hh, b_ih, b_hh, g_mem, b_mem, Wk, Wv, out_0, out_1
+):
+    nc = tc.nc
+    with ExitStack() as ctx:
+        keep = ctx.enter_context(tc.tile_pool(name="keep", bufs=1))
+        tpose = ctx.enter_context(tc.psum_pool(name="tpose", bufs=3))
+        banks = ctx.enter_context(tc.psum_pool(name="banks", bufs=1))
+
+        act_sb = keep.tile([P, 2 * D], BF16, name="act_sb")
+        nc.sync.dma_start(out=act_sb[:, 0:D], in_=agg.rearrange("b s d -> (b s) d"))
+        nc.sync.dma_start(out=act_sb[:, D : 2 * D], in_=M_old.rearrange("b s d -> (b s) d"))
+
+        def load_gate(w, gate, name):
+            rows = keep.tile([P, CHUNKS * D], BF16, name=name)
+            nc.sync.dma_start(
+                out=rows[:],
+                in_=w[gate * D : (gate + 1) * D, :].rearrange("(p c) k -> p (c k)", c=CHUNKS),
+            )
+            return rows
+
+        def load_projection(w, name):
+            rows = keep.tile([P, CHUNKS * D], BF16, name=name)
+            nc.sync.dma_start(
+                out=rows[:].rearrange("p (c k) -> p c k", c=CHUNKS),
+                in_=w.rearrange("(c p) k -> p c k", p=P),
+            )
+            return rows
+
+        R, Z, N = 0, 1, 2
+        ih_r = load_gate(W_ih, R, "ih_r")
+        hh_r = load_gate(W_hh, R, "hh_r")
+        ih_n = load_gate(W_ih, N, "ih_n")
+        hh_n = load_gate(W_hh, N, "hh_n")
+        ih_z = load_gate(W_ih, Z, "ih_z")
+        hh_z = load_gate(W_hh, Z, "hh_z")
+        wk_sb = load_projection(Wk, "wk_sb")
+        wv_sb = load_projection(Wv, "wv_sb")
+
+        bih_raw = keep.tile([P, 3, CHUNKS], BF16, name="bih_raw")
+        bhh_raw = keep.tile([P, 3, CHUNKS], BF16, name="bhh_raw")
+        gain_raw = keep.tile([P, CHUNKS], BF16, name="gain_raw")
+        shift_raw = keep.tile([P, CHUNKS], BF16, name="shift_raw")
+        nc.scalar.dma_start(out=bih_raw[:], in_=b_ih.rearrange("(g p c) -> p g c", g=3, c=CHUNKS))
+        nc.scalar.dma_start(out=bhh_raw[:], in_=b_hh.rearrange("(g p c) -> p g c", g=3, c=CHUNKS))
+        nc.scalar.dma_start(out=gain_raw[:], in_=g_mem.rearrange("(p c) -> p c", c=CHUNKS))
+        nc.scalar.dma_start(out=shift_raw[:], in_=b_mem.rearrange("(p c) -> p c", c=CHUNKS))
+
+        ident = keep.tile([P, P], F32, name="ident")
+        make_identity(nc, ident[:])
+        average = keep.tile([P, P], F32, name="average")
+        nc.vector.memset(average[:], 1.0 / D)
+        eps = keep.tile([P, 1], F32, name="eps")
+        nc.vector.memset(eps[:], EPS)
+
+        b_sum = keep.tile([P, 3, CHUNKS], F32, name="b_sum")
+        nc.vector.tensor_tensor(out=b_sum[:], in0=bih_raw[:], in1=bhh_raw[:], op=ALU.add)
+        b_in = keep.tile([P, CHUNKS], F32, name="b_in")
+        nc.vector.tensor_copy(out=b_in[:], in_=bih_raw[:, N, :])
+        b_hn = keep.tile([P, CHUNKS], F32, name="b_hn")
+        nc.vector.tensor_copy(out=b_hn[:], in_=bhh_raw[:, N, :])
+
+        def transpose_bank(words, grouped_words, consecutive, copy):
+            bank = tpose.tile([P, 2 * 2 * P], F32, name="tp")
+            for c in range(2):
+                for u in range(2):
+                    if consecutive:
+                        src = words[:, c * WORDS + u : (c + 1) * WORDS : 2]
+                    else:
+                        src = words[:, c * WORDS + u * P : c * WORDS + (u + 1) * P]
+                    nc.tensor.transpose(bank[:, (2 * c + u) * P : (2 * c + u + 1) * P], src, ident[:])
+            copy(
+                out=grouped_words.rearrange("q (c r u) -> q c r u", c=2, u=2),
+                in_=bank[:].rearrange("q (c u r) -> q c r u", c=2, u=2),
+            )
+
+        def quantise_rows(rows, name, consecutive, copies):
+            grouped = keep.tile([P, CHUNKS * P * PACK], BF16, name=name + "_grouped", align_bytes=64)
+            codes = keep.tile([P, CHUNKS * P], U32, name=name + "_codes", align_bytes=64)
+            scales = keep.tile([P, CHUNKS * P], U8, name=name + "_scales", align_bytes=64)
+            for half in range(2):
+                transpose_bank(
+                    rows[:].bitcast(F32)[:, half * 2 * WORDS : (half + 1) * 2 * WORDS],
+                    grouped[:].bitcast(F32)[:, half * 2 * WORDS : (half + 1) * 2 * WORDS],
+                    consecutive,
+                    copies[half],
+                )
+                cols = slice(half * 2 * P, (half + 1) * 2 * P)
+                nc.vector.quantize_mx(
+                    out=codes[:, cols].bitcast(FP8X4),
+                    scales=scales[:, cols],
+                    in_=grouped[:, half * 2 * P * PACK : (half + 1) * 2 * P * PACK],
+                )
+            return codes, scales
+
+        act_grouped = keep.tile([P, 2 * P * PACK], BF16, name="act_grouped", align_bytes=64)
+        act_codes = keep.tile([P, 2 * P], U32, name="act_codes", align_bytes=64)
+        act_scales = keep.tile([P, 2 * P], U8, name="act_scales", align_bytes=64)
+        transpose_bank(act_sb[:].bitcast(F32), act_grouped[:].bitcast(F32), False, nc.vector.tensor_copy)
+        nc.vector.quantize_mx(out=act_codes[:].bitcast(FP8X4), scales=act_scales[:], in_=act_grouped[:])
+
+        m_ps = banks.tile([P, 2 * P], F32, name="m_ps", tag="stat")
+        for u in range(2):
+            nc.tensor.transpose(
+                m_ps[:, u * P : (u + 1) * P], act_sb[:].bitcast(F32)[:, WORDS + u : 2 * WORDS : 2], ident[:]
+            )
+        m_t = keep.tile([P, D], F32, name="m_t")
+        nc.vector.tensor_copy(
+            out=m_t[:].rearrange("p (u e s) -> p u e s", u=2, e=2),
+            in_=m_ps[:].bitcast(BF16).rearrange("p (u s e) -> p u e s", u=2, e=2),
+        )
+
+        def gate_product(bank, terms):
+            for c in range(CHUNKS):
+                cols = slice(c * P, (c + 1) * P)
+                for i, ((codes, scales), a) in enumerate(terms):
+                    nc.tensor.matmul_mx(
+                        out=bank[:, cols],
+                        lhsT=codes[:, cols].bitcast(FP8X4),
+                        lhsT_scale=scales[:, cols],
+                        rhs=act_codes[:, a * P : (a + 1) * P].bitcast(FP8X4),
+                        rhs_scale=act_scales[:, a * P : (a + 1) * P],
+                        start=(i == 0),
+                        stop=(i == len(terms) - 1),
+                    )
+
+        def squash(out, bank, func, bias):
+            for c in range(CHUNKS):
+                cols = slice(c * P, (c + 1) * P)
+                nc.scalar.activation(out=out[:, cols], in_=bank[:, cols], func=func, bias=bias[:, c : c + 1])
+
+        AGG, MOLD = 0, 1
+        both = [nc.scalar.copy, nc.vector.tensor_copy]
+        scalar_only = [nc.scalar.copy, nc.scalar.copy]
+
+        q_ih_r = quantise_rows(ih_r, "ih_r", False, scalar_only)
+        q_hh_r = quantise_rows(hh_r, "hh_r", False, both)
+        r_ps = banks.tile([P, D], F32, name="r_ps")
+        gate_product(r_ps, [(q_ih_r, AGG), (q_hh_r, MOLD)])
+        r = keep.tile([P, D], F32, name="r")
+        squash(r, r_ps, ACT.Sigmoid, b_sum[:, R, :])
+
+        q_ih_n = quantise_rows(ih_n, "ih_n", False, scalar_only)
+        q_hh_n = quantise_rows(hh_n, "hh_n", False, both)
+        gin_ps = banks.tile([P, D], F32, name="gin_ps")
+        ghn_ps = banks.tile([P, D], F32, name="ghn_ps")
+        gate_product(ghn_ps, [(q_hh_n, MOLD)])
+        gate_product(gin_ps, [(q_ih_n, AGG)])
+        n_pre = keep.tile([P, D], F32, name="n_pre")
+        for c in range(CHUNKS):
+            cols = slice(c * P, (c + 1) * P)
+            nc.vector.scalar_tensor_tensor(
+                out=n_pre[:, cols], in0=ghn_ps[:, cols], scalar=b_hn[:, c : c + 1], in1=r[:, cols],
+                op0=ALU.add, op1=ALU.mult,
+            )
+        nc.vector.tensor_tensor(out=n_pre[:], in0=gin_ps[:], in1=n_pre[:], op=ALU.add)
+        n = keep.tile([P, D], F32, name="n")
+        squash(n, n_pre, ACT.Tanh, b_in)
+        m_minus_n = keep.tile([P, D], F32, name="m_minus_n")
+        nc.vector.tensor_tensor(out=m_minus_n[:], in0=m_t[:], in1=n[:], op=ALU.subtract)
+
+        q_ih_z = quantise_rows(ih_z, "ih_z", False, scalar_only)
+        q_hh_z = quantise_rows(hh_z, "hh_z", False, both)
+        z_ps = banks.tile([P, D], F32, name="z_ps")
+        gate_product(z_ps, [(q_ih_z, AGG), (q_hh_z, MOLD)])
+        z = keep.tile([P, D], F32, name="z")
+        squash(z, z_ps, ACT.Sigmoid, b_sum[:, Z, :])
+        table_warm = keep.tile([P, 1], F32, name="table_warm")
+        nc.scalar.activation(
+            out=table_warm[:], in_=z[:, D - 1 : D], func=ACT.Abs_reciprocal_sqrt, bias=eps[:, 0:1]
+        )
+        h = keep.tile([P, D], F32, name="h")
+        nc.vector.tensor_tensor(out=h[:], in0=z[:], in1=m_minus_n[:], op=ALU.mult)
+        nc.vector.tensor_tensor(out=h[:], in0=h[:], in1=n[:], op=ALU.add)
+
+        q_k = quantise_rows(wk_sb, "wk", True, scalar_only)
+        q_v = quantise_rows(wv_sb, "wv", True, scalar_only)
+
+        def mean_over_features(out_ps, x):
+            for c in range(CHUNKS):
+                nc.tensor.matmul(
+                    out=out_ps[:], lhsT=average[:], rhs=x[:, c * P : (c + 1) * P],
+                    start=(c == 0), stop=(c == CHUNKS - 1),
+                )
+
+        mean_ps = banks.tile([P, P], F32, name="mean_ps", tag="stat")
+        mean_over_features(mean_ps, h)
+        centred = keep.tile([P, D], F32, name="centred")
+        nc.vector.tensor_tensor(
+            out=centred[:].rearrange("p (c s) -> p c s", c=CHUNKS),
+            in0=h[:].rearrange("p (c s) -> p c s", c=CHUNKS),
+            in1=mean_ps[:].unsqueeze(1).to_broadcast([P, CHUNKS, P]),
+            op=ALU.subtract,
+        )
+        squares = keep.tile([P, D], F32, name="squares")
+        nc.scalar.activation(out=squares[:], in_=centred[:], func=ACT.Square)
+        var_ps = banks.tile([P, P], F32, name="var_ps", tag="stat")
+        mean_over_features(var_ps, squares)
+        rstd = keep.tile([P, P], F32, name="rstd")
+        nc.scalar.activation(out=rstd[:], in_=var_ps[:], func=ACT.Abs_reciprocal_sqrt, bias=eps[:, 0:1])
+
+        scaled = keep.tile([P, D], F32, name="scaled")
+        nc.vector.tensor_tensor(
+            out=scaled[:].rearrange("p (s c) -> p s c", c=CHUNKS),
+            in0=centred[:].rearrange("p (c s) -> p s c", c=CHUNKS),
+            in1=gain_raw[:].unsqueeze(1).to_broadcast([P, P, CHUNKS]),
+            op=ALU.mult,
+        )
+        nc.vector.tensor_tensor(
+            out=scaled[:].rearrange("p (s c) -> p s c", c=CHUNKS),
+            in0=scaled[:].rearrange("p (s c) -> p s c", c=CHUNKS),
+            in1=rstd[:].unsqueeze(2).to_broadcast([P, P, CHUNKS]),
+            op=ALU.mult,
+        )
+        m_new = keep.tile([P, P * PACK], BF16, name="m_new", align_bytes=64)
+        nc.vector.tensor_tensor(
+            out=m_new[:].rearrange("p (s c) -> p s c", c=CHUNKS),
+            in0=scaled[:].rearrange("p (s c) -> p s c", c=CHUNKS),
+            in1=shift_raw[:].unsqueeze(1).to_broadcast([P, P, CHUNKS]),
+            op=ALU.add,
+        )
+        m_codes = keep.tile([P, P], U32, name="m_codes", align_bytes=64)
+        m_scales = keep.tile([P, P], U8, name="m_scales", align_bytes=64)
+        nc.vector.quantize_mx(out=m_codes[:].bitcast(FP8X4), scales=m_scales[:], in_=m_new[:])
+
+        def project(q_w, tag, copy, queue, out):
+            codes, scales = q_w
+            acc = banks.tile([P, D], F32, name="acc_" + tag, tag=tag)
+            nc.tensor.matmul_mx(
+                out=acc[:],
+                lhsT=m_codes[:].bitcast(FP8X4),
+                lhsT_scale=m_scales[:],
+                rhs=codes[:].bitcast(FP8X4),
+                rhs_scale=scales[:],
+                start=True,
+                stop=True,
+            )
+            result = keep.tile([P, D], F32, name="result_" + tag)
+            copy(out=result[:], in_=acc[:])
+            queue.dma_start(out=out.rearrange("b s d -> (b s) d"), in_=result[:])
+
+        project(q_k, "r_ps", nc.scalar.copy, nc.sync, out_0)
+        project(q_v, "ghn_ps", nc.vector.tensor_copy, nc.scalar, out_1)

@@ -14,11 +14,16 @@ ALU = mybir.AluOpType
 P = 128
 D = 512
 PACK = 4
-CHUNKS = D // P
 WORDS = D // 2
 EPS = 1e-5
+R, Z, N = 0, 1, 2
+AGG, MOLD = 0, 1
 
 FLOPS = 2 * P * D * (2 * 3 * D + 2 * D)
+
+
+def chunk(t):
+    return slice(t * P, (t + 1) * P)
 
 
 def tile_instrumentspecificslotmemory_pb_s_kernel(
@@ -26,31 +31,44 @@ def tile_instrumentspecificslotmemory_pb_s_kernel(
 ):
     nc = tc.nc
     with ExitStack() as ctx:
+        ctx.enter_context(tc.manual_schedule())
         keep = ctx.enter_context(tc.tile_pool(name="keep", bufs=1))
-        tpose = ctx.enter_context(tc.psum_pool(name="tpose", bufs=3))
+        tpose = ctx.enter_context(tc.psum_pool(name="tpose", bufs=4))
         banks = ctx.enter_context(tc.psum_pool(name="banks", bufs=1))
+
+        ident = keep.tile([P, P], F32, name="ident")
+        make_identity(nc, ident[:])
+        bias_rows = keep.tile([P, 2 * P], BF16, name="bias_rows")
+        nc.vector.memset(bias_rows[:], 0.0)
+        affine_rows = keep.tile([P, 2 * D], BF16, name="affine_rows")
+        nc.vector.memset(affine_rows[:], 0.0)
+        zero = keep.tile([P, 1], F32, name="zero")
+        nc.vector.memset(zero[:], 0.0)
+        ones = keep.tile([P, P], BF16, name="ones")
+        nc.vector.memset(ones[:], 1.0)
+        minus_half = keep.tile([P, 1], F32, name="minus_half")
+        nc.vector.memset(minus_half[:], -0.5)
 
         act_sb = keep.tile([P, 2 * D], BF16, name="act_sb")
         nc.sync.dma_start(out=act_sb[:, 0:D], in_=agg.rearrange("b s d -> (b s) d"))
         nc.sync.dma_start(out=act_sb[:, D : 2 * D], in_=M_old.rearrange("b s d -> (b s) d"))
 
         def load_gate(w, gate, name):
-            rows = keep.tile([P, CHUNKS * D], BF16, name=name)
+            rows = keep.tile([P, PACK * D], BF16, name=name)
             nc.sync.dma_start(
-                out=rows[:],
-                in_=w[gate * D : (gate + 1) * D, :].rearrange("(p c) k -> p (c k)", c=CHUNKS),
+                out=rows[:].rearrange("p (u x) -> p u x", u=2),
+                in_=w[gate * D : (gate + 1) * D, :].rearrange("(u p e) k -> p u (e k)", u=2, e=2),
             )
             return rows
 
         def load_projection(w, name):
-            rows = keep.tile([P, CHUNKS * D], BF16, name=name)
+            rows = keep.tile([P, PACK * D], BF16, name=name)
             nc.sync.dma_start(
-                out=rows[:].rearrange("p (c k) -> p c k", c=CHUNKS),
+                out=rows[:].rearrange("p (c k) -> p c k", c=PACK),
                 in_=w.rearrange("(c p) k -> p c k", p=P),
             )
             return rows
 
-        R, Z, N = 0, 1, 2
         ih_r = load_gate(W_ih, R, "ih_r")
         hh_r = load_gate(W_hh, R, "hh_r")
         ih_n = load_gate(W_ih, N, "ih_n")
@@ -60,52 +78,33 @@ def tile_instrumentspecificslotmemory_pb_s_kernel(
         wk_sb = load_projection(Wk, "wk_sb")
         wv_sb = load_projection(Wv, "wv_sb")
 
-        bih_raw = keep.tile([P, 3, CHUNKS], BF16, name="bih_raw")
-        bhh_raw = keep.tile([P, 3, CHUNKS], BF16, name="bhh_raw")
-        gain_raw = keep.tile([P, CHUNKS], BF16, name="gain_raw")
-        shift_raw = keep.tile([P, CHUNKS], BF16, name="shift_raw")
-        nc.scalar.dma_start(out=bih_raw[:], in_=b_ih.rearrange("(g p c) -> p g c", g=3, c=CHUNKS))
-        nc.scalar.dma_start(out=bhh_raw[:], in_=b_hh.rearrange("(g p c) -> p g c", g=3, c=CHUNKS))
-        nc.scalar.dma_start(out=gain_raw[:], in_=g_mem.rearrange("(p c) -> p c", c=CHUNKS))
-        nc.scalar.dma_start(out=shift_raw[:], in_=b_mem.rearrange("(p c) -> p c", c=CHUNKS))
+        nc.scalar.dma_start(out=bias_rows[0:6, :], in_=b_ih.rearrange("(j x) -> j x", x=2 * P))
+        nc.scalar.dma_start(out=bias_rows[6:12, :], in_=b_hh.rearrange("(j x) -> j x", x=2 * P))
+        nc.scalar.dma_start(out=affine_rows[0:1, 0:D], in_=g_mem.rearrange("(o d) -> o d", o=1))
+        nc.scalar.dma_start(out=affine_rows[0:1, D : 2 * D], in_=b_mem.rearrange("(o d) -> o d", o=1))
+        table_warm = keep.tile([P, 1], F32, name="table_warm")
+        nc.scalar.activation(out=table_warm[:], in_=zero[:], func=ACT.Sigmoid)
 
-        ident = keep.tile([P, P], F32, name="ident")
-        make_identity(nc, ident[:])
-        average = keep.tile([P, P], F32, name="average")
-        nc.vector.memset(average[:], 1.0 / D)
-        eps = keep.tile([P, 1], F32, name="eps")
-        nc.vector.memset(eps[:], EPS)
-
-        b_sum = keep.tile([P, 3, CHUNKS], F32, name="b_sum")
-        nc.vector.tensor_tensor(out=b_sum[:], in0=bih_raw[:], in1=bhh_raw[:], op=ALU.add)
-        b_in = keep.tile([P, CHUNKS], F32, name="b_in")
-        nc.vector.tensor_copy(out=b_in[:], in_=bih_raw[:, N, :])
-        b_hn = keep.tile([P, CHUNKS], F32, name="b_hn")
-        nc.vector.tensor_copy(out=b_hn[:], in_=bhh_raw[:, N, :])
-
-        def transpose_bank(words, grouped_words, consecutive, copy):
+        def transpose_bank(words, grouped_words, copy):
             bank = tpose.tile([P, 2 * 2 * P], F32, name="tp")
             for c in range(2):
                 for u in range(2):
-                    if consecutive:
-                        src = words[:, c * WORDS + u : (c + 1) * WORDS : 2]
-                    else:
-                        src = words[:, c * WORDS + u * P : c * WORDS + (u + 1) * P]
-                    nc.tensor.transpose(bank[:, (2 * c + u) * P : (2 * c + u + 1) * P], src, ident[:])
+                    nc.tensor.transpose(
+                        bank[:, chunk(2 * c + u)], words[:, c * WORDS + u * P : c * WORDS + (u + 1) * P], ident[:]
+                    )
             copy(
                 out=grouped_words.rearrange("q (c r u) -> q c r u", c=2, u=2),
                 in_=bank[:].rearrange("q (c u r) -> q c r u", c=2, u=2),
             )
 
-        def quantise_rows(rows, name, consecutive, copies):
-            grouped = keep.tile([P, CHUNKS * P * PACK], BF16, name=name + "_grouped", align_bytes=64)
-            codes = keep.tile([P, CHUNKS * P], U32, name=name + "_codes", align_bytes=64)
-            scales = keep.tile([P, CHUNKS * P], U8, name=name + "_scales", align_bytes=64)
+        def quantise_rows(rows, name, copies):
+            grouped = keep.tile([P, PACK * P * PACK], BF16, name=name + "_grouped", align_bytes=64)
+            codes = keep.tile([P, PACK * P], U32, name=name + "_codes", align_bytes=64)
+            scales = keep.tile([P, PACK * P], U8, name=name + "_scales", align_bytes=64)
             for half in range(2):
                 transpose_bank(
                     rows[:].bitcast(F32)[:, half * 2 * WORDS : (half + 1) * 2 * WORDS],
                     grouped[:].bitcast(F32)[:, half * 2 * WORDS : (half + 1) * 2 * WORDS],
-                    consecutive,
                     copies[half],
                 )
                 cols = slice(half * 2 * P, (half + 1) * 2 * P)
@@ -116,137 +115,131 @@ def tile_instrumentspecificslotmemory_pb_s_kernel(
                 )
             return codes, scales
 
+        scalar_only = [nc.scalar.copy, nc.scalar.copy]
+        shared = [nc.scalar.copy, nc.vector.tensor_copy]
+
         act_grouped = keep.tile([P, 2 * P * PACK], BF16, name="act_grouped", align_bytes=64)
         act_codes = keep.tile([P, 2 * P], U32, name="act_codes", align_bytes=64)
         act_scales = keep.tile([P, 2 * P], U8, name="act_scales", align_bytes=64)
-        transpose_bank(act_sb[:].bitcast(F32), act_grouped[:].bitcast(F32), False, nc.vector.tensor_copy)
+        transpose_bank(act_sb[:].bitcast(F32), act_grouped[:].bitcast(F32), nc.vector.tensor_copy)
         nc.vector.quantize_mx(out=act_codes[:].bitcast(FP8X4), scales=act_scales[:], in_=act_grouped[:])
-
-        m_ps = banks.tile([P, 2 * P], F32, name="m_ps", tag="stat")
-        for u in range(2):
-            nc.tensor.transpose(
-                m_ps[:, u * P : (u + 1) * P], act_sb[:].bitcast(F32)[:, WORDS + u : 2 * WORDS : 2], ident[:]
-            )
-        m_t = keep.tile([P, D], F32, name="m_t")
-        nc.vector.tensor_copy(
-            out=m_t[:].rearrange("p (u e s) -> p u e s", u=2, e=2),
-            in_=m_ps[:].bitcast(BF16).rearrange("p (u s e) -> p u e s", u=2, e=2),
-        )
+        m_t = act_grouped[:, MOLD * P * PACK : (MOLD + 1) * P * PACK].rearrange("q (s t) -> q t s", t=PACK)
 
         def gate_product(bank, terms):
-            for c in range(CHUNKS):
-                cols = slice(c * P, (c + 1) * P)
+            for t in range(PACK):
                 for i, ((codes, scales), a) in enumerate(terms):
                     nc.tensor.matmul_mx(
-                        out=bank[:, cols],
-                        lhsT=codes[:, cols].bitcast(FP8X4),
-                        lhsT_scale=scales[:, cols],
-                        rhs=act_codes[:, a * P : (a + 1) * P].bitcast(FP8X4),
-                        rhs_scale=act_scales[:, a * P : (a + 1) * P],
+                        out=bank[:, chunk(t)],
+                        lhsT=codes[:, chunk(t)].bitcast(FP8X4),
+                        lhsT_scale=scales[:, chunk(t)],
+                        rhs=act_codes[:, chunk(a)].bitcast(FP8X4),
+                        rhs_scale=act_scales[:, chunk(a)],
                         start=(i == 0),
                         stop=(i == len(terms) - 1),
                     )
 
-        def squash(out, bank, func, bias):
-            for c in range(CHUNKS):
-                cols = slice(c * P, (c + 1) * P)
-                nc.scalar.activation(out=out[:, cols], in_=bank[:, cols], func=func, bias=bias[:, c : c + 1])
+        def squash(out, pre, func, bias):
+            for t in range(PACK):
+                nc.scalar.activation(out=out[:, chunk(t)], in_=pre[:, chunk(t)], func=func, bias=bias[:, t : t + 1])
 
-        AGG, MOLD = 0, 1
-        both = [nc.scalar.copy, nc.vector.tensor_copy]
-        scalar_only = [nc.scalar.copy, nc.scalar.copy]
+        q_ih_r = quantise_rows(ih_r, "ih_r", scalar_only)
 
-        q_ih_r = quantise_rows(ih_r, "ih_r", False, scalar_only)
-        q_hh_r = quantise_rows(hh_r, "hh_r", False, both)
+        bias_ps = banks.tile([P, P], F32, name="bias_ps", tag="z_ps")
+        nc.tensor.transpose(bias_ps[:], bias_rows[:].bitcast(F32), ident[:])
+        gain_ps = banks.tile([P, D], F32, name="gain_ps", tag="gin_ps")
+        shift_ps = banks.tile([P, D], F32, name="shift_ps", tag="ghn_ps")
+        nc.tensor.matmul(out=gain_ps[:], lhsT=ones[:], rhs=affine_rows[:, 0:D], start=True, stop=True)
+        nc.tensor.matmul(out=shift_ps[:], lhsT=ones[:], rhs=affine_rows[:, D : 2 * D], start=True, stop=True)
+        bias = keep.tile([P, 2, 3, PACK], F32, name="bias")
+        nc.vector.tensor_copy(
+            out=bias[:].rearrange("q a g t -> q (a g t)"), in_=bias_ps[:].bitcast(BF16)[:, 0 : 2 * 3 * PACK]
+        )
+        bias_sum = keep.tile([P, 3, PACK], F32, name="bias_sum")
+        nc.vector.tensor_tensor(out=bias_sum[:], in0=bias[:, 0, :, :], in1=bias[:, 1, :, :], op=ALU.add)
+
+        q_hh_r = quantise_rows(hh_r, "hh_r", shared)
+
+        gain = keep.tile([P, D], F32, name="gain")
+        shift = keep.tile([P, D], F32, name="shift")
+        for spread, bank in ((gain, gain_ps), (shift, shift_ps)):
+            nc.vector.tensor_copy(
+                out=spread[:].rearrange("s (u e q) -> s u e q", u=2, e=2),
+                in_=bank[:].rearrange("s (u q e) -> s u e q", u=2, e=2),
+            )
+
+        q_ih_n = quantise_rows(ih_n, "ih_n", scalar_only)
+
         r_ps = banks.tile([P, D], F32, name="r_ps")
         gate_product(r_ps, [(q_ih_r, AGG), (q_hh_r, MOLD)])
         r = keep.tile([P, D], F32, name="r")
-        squash(r, r_ps, ACT.Sigmoid, b_sum[:, R, :])
+        squash(r, r_ps, ACT.Sigmoid, bias_sum[:, R, :])
 
-        q_ih_n = quantise_rows(ih_n, "ih_n", False, scalar_only)
-        q_hh_n = quantise_rows(hh_n, "hh_n", False, both)
+        q_hh_n = quantise_rows(hh_n, "hh_n", shared)
+        q_ih_z = quantise_rows(ih_z, "ih_z", scalar_only)
+        q_hh_z = quantise_rows(hh_z, "hh_z", shared)
+
         gin_ps = banks.tile([P, D], F32, name="gin_ps")
         ghn_ps = banks.tile([P, D], F32, name="ghn_ps")
         gate_product(ghn_ps, [(q_hh_n, MOLD)])
         gate_product(gin_ps, [(q_ih_n, AGG)])
         n_pre = keep.tile([P, D], F32, name="n_pre")
-        for c in range(CHUNKS):
-            cols = slice(c * P, (c + 1) * P)
+        for t in range(PACK):
             nc.vector.scalar_tensor_tensor(
-                out=n_pre[:, cols], in0=ghn_ps[:, cols], scalar=b_hn[:, c : c + 1], in1=r[:, cols],
+                out=n_pre[:, chunk(t)], in0=ghn_ps[:, chunk(t)], scalar=bias[:, 1, N, t : t + 1], in1=r[:, chunk(t)],
                 op0=ALU.add, op1=ALU.mult,
             )
         nc.vector.tensor_tensor(out=n_pre[:], in0=gin_ps[:], in1=n_pre[:], op=ALU.add)
-        n = keep.tile([P, D], F32, name="n")
-        squash(n, n_pre, ACT.Tanh, b_in)
-        m_minus_n = keep.tile([P, D], F32, name="m_minus_n")
-        nc.vector.tensor_tensor(out=m_minus_n[:], in0=m_t[:], in1=n[:], op=ALU.subtract)
 
-        q_ih_z = quantise_rows(ih_z, "ih_z", False, scalar_only)
-        q_hh_z = quantise_rows(hh_z, "hh_z", False, both)
         z_ps = banks.tile([P, D], F32, name="z_ps")
         gate_product(z_ps, [(q_ih_z, AGG), (q_hh_z, MOLD)])
         z = keep.tile([P, D], F32, name="z")
-        squash(z, z_ps, ACT.Sigmoid, b_sum[:, Z, :])
-        table_warm = keep.tile([P, 1], F32, name="table_warm")
-        nc.scalar.activation(
-            out=table_warm[:], in_=z[:, D - 1 : D], func=ACT.Abs_reciprocal_sqrt, bias=eps[:, 0:1]
-        )
+        squash(z, z_ps, ACT.Sigmoid, bias_sum[:, Z, :])
+
+        n = keep.tile([P, D], F32, name="n")
+        squash(n, n_pre, ACT.Tanh, bias[:, 0, N, :])
         h = keep.tile([P, D], F32, name="h")
-        nc.vector.tensor_tensor(out=h[:], in0=z[:], in1=m_minus_n[:], op=ALU.mult)
-        nc.vector.tensor_tensor(out=h[:], in0=h[:], in1=n[:], op=ALU.add)
-
-        q_k = quantise_rows(wk_sb, "wk", True, scalar_only)
-        q_v = quantise_rows(wv_sb, "wv", True, scalar_only)
-
-        def mean_over_features(out_ps, x):
-            for c in range(CHUNKS):
-                nc.tensor.matmul(
-                    out=out_ps[:], lhsT=average[:], rhs=x[:, c * P : (c + 1) * P],
-                    start=(c == 0), stop=(c == CHUNKS - 1),
-                )
-
-        mean_ps = banks.tile([P, P], F32, name="mean_ps", tag="stat")
-        mean_over_features(mean_ps, h)
-        centred = keep.tile([P, D], F32, name="centred")
         nc.vector.tensor_tensor(
-            out=centred[:].rearrange("p (c s) -> p c s", c=CHUNKS),
-            in0=h[:].rearrange("p (c s) -> p c s", c=CHUNKS),
-            in1=mean_ps[:].unsqueeze(1).to_broadcast([P, CHUNKS, P]),
+            out=h[:].rearrange("q (t s) -> q t s", t=PACK), in0=m_t, in1=n[:].rearrange("q (t s) -> q t s", t=PACK),
             op=ALU.subtract,
         )
-        squares = keep.tile([P, D], F32, name="squares")
-        nc.scalar.activation(out=squares[:], in_=centred[:], func=ACT.Square)
-        var_ps = banks.tile([P, P], F32, name="var_ps", tag="stat")
-        mean_over_features(var_ps, squares)
-        rstd = keep.tile([P, P], F32, name="rstd")
-        nc.scalar.activation(out=rstd[:], in_=var_ps[:], func=ACT.Abs_reciprocal_sqrt, bias=eps[:, 0:1])
+        nc.vector.tensor_tensor(out=h[:], in0=z[:], in1=h[:], op=ALU.mult)
+        nc.vector.tensor_tensor(out=h[:], in0=h[:], in1=n[:], op=ALU.add)
 
-        scaled = keep.tile([P, D], F32, name="scaled")
-        nc.vector.tensor_tensor(
-            out=scaled[:].rearrange("p (s c) -> p s c", c=CHUNKS),
-            in0=centred[:].rearrange("p (c s) -> p s c", c=CHUNKS),
-            in1=gain_raw[:].unsqueeze(1).to_broadcast([P, P, CHUNKS]),
-            op=ALU.mult,
+        q_k = quantise_rows(wk_sb, "wk", scalar_only)
+        q_v = quantise_rows(wv_sb, "wv", scalar_only)
+
+        h_ps = banks.tile([P, D], F32, name="h_ps", tag="r_ps")
+        for t in range(PACK):
+            nc.tensor.transpose(h_ps[:, chunk(t)], h[:, chunk(t)], ident[:])
+        stats = keep.tile([P, 6], F32, name="stats")
+        nc.vector.bn_stats(out=stats[:], in_=h_ps[:])
+        mean_var = keep.tile([P, 2], F32, name="mean_var")
+        nc.vector.bn_aggr(out=mean_var[:], in_=stats[:])
+        var_eps = keep.tile([P, 1], F32, name="var_eps")
+        nc.vector.tensor_scalar_add(out=var_eps[:], in0=mean_var[:, 1:2], scalar1=EPS)
+        rstd = keep.tile([P, 1], F32, name="rstd")
+        nc.gpsimd.tensor_tensor(out=rstd[:], in0=var_eps[:], in1=minus_half[:], op=ALU.pow)
+        m_new = keep.tile([P, D], F32, name="m_new")
+        nc.vector.scalar_tensor_tensor(
+            out=m_new[:], in0=h_ps[:], scalar=mean_var[:, 0:1], in1=gain[:], op0=ALU.subtract, op1=ALU.mult
         )
-        nc.vector.tensor_tensor(
-            out=scaled[:].rearrange("p (s c) -> p s c", c=CHUNKS),
-            in0=scaled[:].rearrange("p (s c) -> p s c", c=CHUNKS),
-            in1=rstd[:].unsqueeze(2).to_broadcast([P, P, CHUNKS]),
-            op=ALU.mult,
+        nc.vector.scalar_tensor_tensor(
+            out=m_new[:], in0=m_new[:], scalar=rstd[:, 0:1], in1=shift[:], op0=ALU.mult, op1=ALU.add
         )
-        m_new = keep.tile([P, P * PACK], BF16, name="m_new", align_bytes=64)
-        nc.vector.tensor_tensor(
-            out=m_new[:].rearrange("p (s c) -> p s c", c=CHUNKS),
-            in0=scaled[:].rearrange("p (s c) -> p s c", c=CHUNKS),
-            in1=shift_raw[:].unsqueeze(1).to_broadcast([P, P, CHUNKS]),
-            op=ALU.add,
+
+        m_new_ps = banks.tile([P, D], F32, name="m_new_ps", tag="ghn_ps")
+        for t in range(PACK):
+            nc.tensor.transpose(m_new_ps[:, chunk(t)], m_new[:, chunk(t)], ident[:])
+        m_grouped = keep.tile([P, P * PACK], BF16, name="m_grouped", align_bytes=64)
+        nc.scalar.copy(
+            out=m_grouped[:].rearrange("q (s t) -> q s t", t=PACK),
+            in_=m_new_ps[:].rearrange("q (t s) -> q s t", t=PACK),
         )
         m_codes = keep.tile([P, P], U32, name="m_codes", align_bytes=64)
         m_scales = keep.tile([P, P], U8, name="m_scales", align_bytes=64)
-        nc.vector.quantize_mx(out=m_codes[:].bitcast(FP8X4), scales=m_scales[:], in_=m_new[:])
+        nc.vector.quantize_mx(out=m_codes[:].bitcast(FP8X4), scales=m_scales[:], in_=m_grouped[:])
 
-        def project(q_w, tag, copy, queue, out):
+        def project(q_w, tag):
             codes, scales = q_w
             acc = banks.tile([P, D], F32, name="acc_" + tag, tag=tag)
             nc.tensor.matmul_mx(
@@ -258,9 +251,13 @@ def tile_instrumentspecificslotmemory_pb_s_kernel(
                 start=True,
                 stop=True,
             )
-            result = keep.tile([P, D], F32, name="result_" + tag)
-            copy(out=result[:], in_=acc[:])
-            queue.dma_start(out=out.rearrange("b s d -> (b s) d"), in_=result[:])
+            return acc
 
-        project(q_k, "r_ps", nc.scalar.copy, nc.sync, out_0)
-        project(q_v, "ghn_ps", nc.vector.tensor_copy, nc.scalar, out_1)
+        kt_ps = project(q_k, "gin_ps")
+        v_ps = project(q_v, "z_ps")
+        kt_sb = keep.tile([P, D], F32, name="kt_sb")
+        v_sb = keep.tile([P, D], F32, name="v_sb")
+        nc.scalar.copy(out=kt_sb[:], in_=kt_ps[:])
+        nc.vector.tensor_copy(out=v_sb[:], in_=v_ps[:])
+        nc.sync.dma_start(out=out_0.rearrange("b s d -> (b s) d"), in_=kt_sb[:])
+        nc.scalar.dma_start(out=out_1.rearrange("b s d -> (b s) d"), in_=v_sb[:])

@@ -14,6 +14,7 @@ ALU = mybir.AluOpType
 P = 128
 D = 512
 PACK = 4
+HALF = D // 2
 WORDS = D // 2
 EPS = 1e-5
 R, Z, N = 0, 1, 2
@@ -24,6 +25,10 @@ FLOPS = 2 * P * D * (2 * 3 * D + 2 * D)
 
 def chunk(t):
     return slice(t * P, (t + 1) * P)
+
+
+def half(u):
+    return slice(u * HALF, (u + 1) * HALF)
 
 
 def tile_instrumentspecificslotmemory_pb_s_kernel(
@@ -40,12 +45,8 @@ def tile_instrumentspecificslotmemory_pb_s_kernel(
         make_identity(nc, ident[:])
         bias_rows = keep.tile([P, 2 * P], BF16, name="bias_rows")
         nc.vector.memset(bias_rows[:], 0.0)
-        affine_rows = keep.tile([P, 2 * D], BF16, name="affine_rows")
-        nc.vector.memset(affine_rows[:], 0.0)
         zero = keep.tile([P, 1], F32, name="zero")
         nc.vector.memset(zero[:], 0.0)
-        ones = keep.tile([P, P], BF16, name="ones")
-        nc.vector.memset(ones[:], 1.0)
         minus_half = keep.tile([P, 1], F32, name="minus_half")
         nc.vector.memset(minus_half[:], -0.5)
 
@@ -54,19 +55,21 @@ def tile_instrumentspecificslotmemory_pb_s_kernel(
         nc.sync.dma_start(out=act_sb[:, D : 2 * D], in_=M_old.rearrange("b s d -> (b s) d"))
 
         def load_gate(w, gate, name):
-            rows = keep.tile([P, PACK * D], BF16, name=name)
-            nc.sync.dma_start(
-                out=rows[:].rearrange("p (u x) -> p u x", u=2),
-                in_=w[gate * D : (gate + 1) * D, :].rearrange("(u p e) k -> p u (e k)", u=2, e=2),
-            )
+            rows = keep.tile([P, 2, 2 * D], BF16, name=name)
+            for u in range(2):
+                first = gate * D + u * HALF
+                nc.sync.dma_start(
+                    out=rows[:, u, :], in_=w[first : first + HALF, :].rearrange("(p e) k -> p (e k)", e=2)
+                )
             return rows
 
         def load_projection(w, name):
-            rows = keep.tile([P, PACK * D], BF16, name=name)
-            nc.sync.dma_start(
-                out=rows[:].rearrange("p (c k) -> p c k", c=PACK),
-                in_=w.rearrange("(c p) k -> p c k", p=P),
-            )
+            rows = keep.tile([P, 2, 2 * D], BF16, name=name)
+            for u in range(2):
+                nc.sync.dma_start(
+                    out=rows[:, u, :].rearrange("p (c k) -> p c k", c=2),
+                    in_=w[u * HALF : (u + 1) * HALF, :].rearrange("(c p) k -> p c k", p=P),
+                )
             return rows
 
         ih_r = load_gate(W_ih, R, "ih_r")
@@ -77,59 +80,54 @@ def tile_instrumentspecificslotmemory_pb_s_kernel(
         hh_z = load_gate(W_hh, Z, "hh_z")
         wk_sb = load_projection(Wk, "wk_sb")
         wv_sb = load_projection(Wv, "wv_sb")
+        gain = keep.tile([P, D], BF16, name="gain")
+        shift = keep.tile([P, D], BF16, name="shift")
+        nc.sync.dma_start(out=gain[:], in_=g_mem.partition_broadcast(P))
+        nc.sync.dma_start(out=shift[:], in_=b_mem.partition_broadcast(P))
 
         nc.scalar.dma_start(out=bias_rows[0:6, :], in_=b_ih.rearrange("(j x) -> j x", x=2 * P))
         nc.scalar.dma_start(out=bias_rows[6:12, :], in_=b_hh.rearrange("(j x) -> j x", x=2 * P))
-        nc.scalar.dma_start(out=affine_rows[0:1, 0:D], in_=g_mem.rearrange("(o d) -> o d", o=1))
-        nc.scalar.dma_start(out=affine_rows[0:1, D : 2 * D], in_=b_mem.rearrange("(o d) -> o d", o=1))
         table_warm = keep.tile([P, 1], F32, name="table_warm")
         nc.scalar.activation(out=table_warm[:], in_=zero[:], func=ACT.Sigmoid)
 
-        def transpose_bank(words, grouped_words, copy):
+        def transpose(words):
             bank = tpose.tile([P, 2 * 2 * P], F32, name="tp")
             for c in range(2):
                 for u in range(2):
                     nc.tensor.transpose(
                         bank[:, chunk(2 * c + u)], words[:, c * WORDS + u * P : c * WORDS + (u + 1) * P], ident[:]
                     )
+            return bank
+
+        def quantise(bank, copy, grouped, codes, scales):
             copy(
-                out=grouped_words.rearrange("q (c r u) -> q c r u", c=2, u=2),
+                out=grouped.bitcast(F32).rearrange("q (c r u) -> q c r u", c=2, u=2),
                 in_=bank[:].rearrange("q (c u r) -> q c r u", c=2, u=2),
             )
+            nc.vector.quantize_mx(out=codes.bitcast(FP8X4), scales=scales, in_=grouped)
 
-        def quantise_rows(rows, name, copies):
-            grouped = keep.tile([P, PACK * P * PACK], BF16, name=name + "_grouped", align_bytes=64)
-            codes = keep.tile([P, PACK * P], U32, name=name + "_codes", align_bytes=64)
-            scales = keep.tile([P, PACK * P], U8, name=name + "_scales", align_bytes=64)
-            for half in range(2):
-                transpose_bank(
-                    rows[:].bitcast(F32)[:, half * 2 * WORDS : (half + 1) * 2 * WORDS],
-                    grouped[:].bitcast(F32)[:, half * 2 * WORDS : (half + 1) * 2 * WORDS],
-                    copies[half],
-                )
-                cols = slice(half * 2 * P, (half + 1) * 2 * P)
-                nc.vector.quantize_mx(
-                    out=codes[:, cols].bitcast(FP8X4),
-                    scales=scales[:, cols],
-                    in_=grouped[:, half * 2 * P * PACK : (half + 1) * 2 * P * PACK],
-                )
-            return codes, scales
+        def operand(name):
+            grouped = keep.tile([P, D * PACK], BF16, name=name + "_grouped", align_bytes=64)
+            codes = keep.tile([P, D], U32, name=name + "_codes", align_bytes=64)
+            scales = keep.tile([P, D], U8, name=name + "_scales", align_bytes=64)
+            return grouped, codes, scales
 
-        scalar_only = [nc.scalar.copy, nc.scalar.copy]
-        shared = [nc.scalar.copy, nc.vector.tensor_copy]
+        def prepare(rows, tiles, u, copy):
+            grouped, codes, scales = tiles
+            bank = transpose(rows[:, u, :].bitcast(F32))
+            quantise(bank, copy, grouped[:, u * HALF * PACK : (u + 1) * HALF * PACK], codes[:, half(u)], scales[:, half(u)])
 
         act_grouped = keep.tile([P, 2 * P * PACK], BF16, name="act_grouped", align_bytes=64)
         act_codes = keep.tile([P, 2 * P], U32, name="act_codes", align_bytes=64)
         act_scales = keep.tile([P, 2 * P], U8, name="act_scales", align_bytes=64)
-        transpose_bank(act_sb[:].bitcast(F32), act_grouped[:].bitcast(F32), nc.vector.tensor_copy)
-        nc.vector.quantize_mx(out=act_codes[:].bitcast(FP8X4), scales=act_scales[:], in_=act_grouped[:])
+        quantise(transpose(act_sb[:].bitcast(F32)), nc.vector.tensor_copy, act_grouped[:], act_codes[:], act_scales[:])
         m_t = act_grouped[:, MOLD * P * PACK : (MOLD + 1) * P * PACK].rearrange("q (s t) -> q t s", t=PACK)
 
-        def gate_product(bank, terms):
-            for t in range(PACK):
-                for i, ((codes, scales), a) in enumerate(terms):
+        def gate_product(bank, first, chunks, terms):
+            for t in chunks:
+                for i, ((grouped, codes, scales), a) in enumerate(terms):
                     nc.tensor.matmul_mx(
-                        out=bank[:, chunk(t)],
+                        out=bank[:, chunk(t - first)],
                         lhsT=codes[:, chunk(t)].bitcast(FP8X4),
                         lhsT_scale=scales[:, chunk(t)],
                         rhs=act_codes[:, chunk(a)].bitcast(FP8X4),
@@ -138,18 +136,17 @@ def tile_instrumentspecificslotmemory_pb_s_kernel(
                         stop=(i == len(terms) - 1),
                     )
 
-        def squash(out, pre, func, bias):
-            for t in range(PACK):
-                nc.scalar.activation(out=out[:, chunk(t)], in_=pre[:, chunk(t)], func=func, bias=bias[:, t : t + 1])
+        q_ih_r, q_hh_r = operand("ih_r"), operand("hh_r")
+        q_ih_n, q_hh_n = operand("ih_n"), operand("hh_n")
+        q_ih_z, q_hh_z = operand("ih_z"), operand("hh_z")
+        q_k, q_v = operand("wk"), operand("wv")
 
-        q_ih_r = quantise_rows(ih_r, "ih_r", scalar_only)
+        for u in range(2):
+            prepare(ih_r, q_ih_r, u, nc.scalar.copy)
+            prepare(hh_r, q_hh_r, u, nc.scalar.copy)
 
-        bias_ps = banks.tile([P, P], F32, name="bias_ps", tag="z_ps")
+        bias_ps = banks.tile([P, P], F32, name="bias_ps", tag="b")
         nc.tensor.transpose(bias_ps[:], bias_rows[:].bitcast(F32), ident[:])
-        gain_ps = banks.tile([P, D], F32, name="gain_ps", tag="gin_ps")
-        shift_ps = banks.tile([P, D], F32, name="shift_ps", tag="ghn_ps")
-        nc.tensor.matmul(out=gain_ps[:], lhsT=ones[:], rhs=affine_rows[:, 0:D], start=True, stop=True)
-        nc.tensor.matmul(out=shift_ps[:], lhsT=ones[:], rhs=affine_rows[:, D : 2 * D], start=True, stop=True)
         bias = keep.tile([P, 2, 3, PACK], F32, name="bias")
         nc.vector.tensor_copy(
             out=bias[:].rearrange("q a g t -> q (a g t)"), in_=bias_ps[:].bitcast(BF16)[:, 0 : 2 * 3 * PACK]
@@ -157,31 +154,26 @@ def tile_instrumentspecificslotmemory_pb_s_kernel(
         bias_sum = keep.tile([P, 3, PACK], F32, name="bias_sum")
         nc.vector.tensor_tensor(out=bias_sum[:], in0=bias[:, 0, :, :], in1=bias[:, 1, :, :], op=ALU.add)
 
-        q_hh_r = quantise_rows(hh_r, "hh_r", shared)
+        prepare(ih_n, q_ih_n, 0, nc.scalar.copy)
+        prepare(hh_n, q_hh_n, 0, nc.scalar.copy)
 
-        gain = keep.tile([P, D], F32, name="gain")
-        shift = keep.tile([P, D], F32, name="shift")
-        for spread, bank in ((gain, gain_ps), (shift, shift_ps)):
-            nc.vector.tensor_copy(
-                out=spread[:].rearrange("s (u e q) -> s u e q", u=2, e=2),
-                in_=bank[:].rearrange("s (u q e) -> s u e q", u=2, e=2),
+        r_ps = banks.tile([P, D], F32, name="r_ps", tag="a")
+        gate_product(r_ps, 0, range(PACK), [(q_ih_r, AGG), (q_hh_r, MOLD)])
+        r = keep.tile([P, D], F32, name="r")
+        for t in range(PACK):
+            nc.scalar.activation(
+                out=r[:, chunk(t)], in_=r_ps[:, chunk(t)], func=ACT.Sigmoid, bias=bias_sum[:, R, t : t + 1]
             )
 
-        q_ih_n = quantise_rows(ih_n, "ih_n", scalar_only)
+        prepare(ih_n, q_ih_n, 1, nc.scalar.copy)
+        prepare(hh_n, q_hh_n, 1, nc.scalar.copy)
+        prepare(ih_z, q_ih_z, 0, nc.scalar.copy)
+        prepare(hh_z, q_hh_z, 0, nc.scalar.copy)
 
-        r_ps = banks.tile([P, D], F32, name="r_ps")
-        gate_product(r_ps, [(q_ih_r, AGG), (q_hh_r, MOLD)])
-        r = keep.tile([P, D], F32, name="r")
-        squash(r, r_ps, ACT.Sigmoid, bias_sum[:, R, :])
-
-        q_hh_n = quantise_rows(hh_n, "hh_n", shared)
-        q_ih_z = quantise_rows(ih_z, "ih_z", scalar_only)
-        q_hh_z = quantise_rows(hh_z, "hh_z", shared)
-
-        gin_ps = banks.tile([P, D], F32, name="gin_ps")
-        ghn_ps = banks.tile([P, D], F32, name="ghn_ps")
-        gate_product(ghn_ps, [(q_hh_n, MOLD)])
-        gate_product(gin_ps, [(q_ih_n, AGG)])
+        gin_ps = banks.tile([P, D], F32, name="gin_ps", tag="c")
+        ghn_ps = banks.tile([P, D], F32, name="ghn_ps", tag="d")
+        gate_product(ghn_ps, 0, range(PACK), [(q_hh_n, MOLD)])
+        gate_product(gin_ps, 0, range(PACK), [(q_ih_n, AGG)])
         n_pre = keep.tile([P, D], F32, name="n_pre")
         for t in range(PACK):
             nc.vector.scalar_tensor_tensor(
@@ -190,46 +182,81 @@ def tile_instrumentspecificslotmemory_pb_s_kernel(
             )
         nc.vector.tensor_tensor(out=n_pre[:], in0=gin_ps[:], in1=n_pre[:], op=ALU.add)
 
-        z_ps = banks.tile([P, D], F32, name="z_ps")
-        gate_product(z_ps, [(q_ih_z, AGG), (q_hh_z, MOLD)])
-        z = keep.tile([P, D], F32, name="z")
-        squash(z, z_ps, ACT.Sigmoid, bias_sum[:, Z, :])
+        prepare(ih_z, q_ih_z, 1, nc.scalar.copy)
+        prepare(hh_z, q_hh_z, 1, nc.vector.tensor_copy)
 
         n = keep.tile([P, D], F32, name="n")
-        squash(n, n_pre, ACT.Tanh, bias[:, 0, N, :])
-        h = keep.tile([P, D], F32, name="h")
-        nc.vector.tensor_tensor(
-            out=h[:].rearrange("q (t s) -> q t s", t=PACK), in0=m_t, in1=n[:].rearrange("q (t s) -> q t s", t=PACK),
-            op=ALU.subtract,
-        )
-        nc.vector.tensor_tensor(out=h[:], in0=z[:], in1=h[:], op=ALU.mult)
-        nc.vector.tensor_tensor(out=h[:], in0=h[:], in1=n[:], op=ALU.add)
-
-        q_k = quantise_rows(wk_sb, "wk", scalar_only)
-        q_v = quantise_rows(wv_sb, "wv", scalar_only)
-
-        h_ps = banks.tile([P, D], F32, name="h_ps", tag="r_ps")
         for t in range(PACK):
-            nc.tensor.transpose(h_ps[:, chunk(t)], h[:, chunk(t)], ident[:])
-        stats = keep.tile([P, 6], F32, name="stats")
-        nc.vector.bn_stats(out=stats[:], in_=h_ps[:])
+            nc.scalar.activation(
+                out=n[:, chunk(t)], in_=n_pre[:, chunk(t)], func=ACT.Tanh, bias=bias[:, 0, N, t : t + 1]
+            )
+
+        z = keep.tile([P, D], F32, name="z")
+        wk_banks = []
+        for u, tag in ((0, "b"), (1, "a")):
+            wk_banks.append(transpose(wk_sb[:, u, :].bitcast(F32)))
+            z_ps = banks.tile([P, HALF], F32, name="z_ps", tag=tag)
+            gate_product(z_ps, 2 * u, (2 * u, 2 * u + 1), [(q_ih_z, AGG), (q_hh_z, MOLD)])
+            for t in (2 * u, 2 * u + 1):
+                nc.scalar.activation(
+                    out=z[:, chunk(t)], in_=z_ps[:, chunk(t - 2 * u)], func=ACT.Sigmoid, bias=bias_sum[:, Z, t : t + 1]
+                )
+            if u == 0:
+                m_minus_n = keep.tile([P, D], F32, name="m_minus_n")
+                nc.vector.tensor_tensor(
+                    out=m_minus_n[:].rearrange("q (t s) -> q t s", t=PACK), in0=m_t,
+                    in1=n[:].rearrange("q (t s) -> q t s", t=PACK), op=ALU.subtract,
+                )
+
+        h = keep.tile([P, D], F32, name="h")
+        h_ps = []
+        for u, tag in ((0, "c"), (1, "d")):
+            nc.vector.tensor_tensor(out=h[:, half(u)], in0=z[:, half(u)], in1=m_minus_n[:, half(u)], op=ALU.mult)
+            nc.vector.tensor_tensor(out=h[:, half(u)], in0=h[:, half(u)], in1=n[:, half(u)], op=ALU.add)
+            h_ps.append(banks.tile([P, HALF], F32, name="h_ps", tag=tag))
+            for e in range(2):
+                nc.tensor.transpose(h_ps[u][:, chunk(e)], h[:, chunk(2 * u + e)], ident[:])
+
+        def quantise_projection(bank, tiles, u):
+            grouped, codes, scales = tiles
+            quantise(bank, nc.scalar.copy, grouped[:, u * HALF * PACK : (u + 1) * HALF * PACK], codes[:, half(u)], scales[:, half(u)])
+
+        wv_banks = [transpose(wv_sb[:, u, :].bitcast(F32)) for u in range(2)]
+
+        stats = keep.tile([P, 2, 6], F32, name="stats")
+        nc.vector.bn_stats(out=stats[:, 0, :], in_=h_ps[0][:])
+        quantise_projection(wk_banks[0], q_k, 0)
+        nc.vector.bn_stats(out=stats[:, 1, :], in_=h_ps[1][:])
         mean_var = keep.tile([P, 2], F32, name="mean_var")
-        nc.vector.bn_aggr(out=mean_var[:], in_=stats[:])
+        nc.vector.bn_aggr(out=mean_var[:], in_=stats[:].rearrange("s u x -> s (u x)"))
         var_eps = keep.tile([P, 1], F32, name="var_eps")
         nc.vector.tensor_scalar_add(out=var_eps[:], in0=mean_var[:, 1:2], scalar1=EPS)
         rstd = keep.tile([P, 1], F32, name="rstd")
         nc.gpsimd.tensor_tensor(out=rstd[:], in0=var_eps[:], in1=minus_half[:], op=ALU.pow)
         m_new = keep.tile([P, D], F32, name="m_new")
-        nc.vector.scalar_tensor_tensor(
-            out=m_new[:], in0=h_ps[:], scalar=mean_var[:, 0:1], in1=gain[:], op0=ALU.subtract, op1=ALU.mult
-        )
-        nc.vector.scalar_tensor_tensor(
-            out=m_new[:], in0=m_new[:], scalar=rstd[:, 0:1], in1=shift[:], op0=ALU.mult, op1=ALU.add
-        )
+        for u in range(2):
+            nc.vector.scalar_tensor_tensor(
+                out=m_new[:, half(u)].rearrange("s (e q) -> s e q", e=2),
+                in0=h_ps[u][:].rearrange("s (e q) -> s e q", e=2),
+                scalar=mean_var[:, 0:1],
+                in1=gain[:, half(u)].rearrange("s (q e) -> s e q", e=2),
+                op0=ALU.subtract, op1=ALU.mult,
+            )
+        quantise_projection(wk_banks[1], q_k, 1)
+        m_new_ps = banks.tile([P, D], F32, name="m_new_ps", tag="b")
+        for u in range(2):
+            nc.vector.scalar_tensor_tensor(
+                out=m_new[:, half(u)].rearrange("s (e q) -> s e q", e=2),
+                in0=m_new[:, half(u)].rearrange("s (e q) -> s e q", e=2),
+                scalar=rstd[:, 0:1],
+                in1=shift[:, half(u)].rearrange("s (q e) -> s e q", e=2),
+                op0=ALU.mult, op1=ALU.add,
+            )
+            for e in range(2):
+                nc.tensor.transpose(m_new_ps[:, chunk(2 * u + e)], m_new[:, chunk(2 * u + e)], ident[:])
+        quantise_projection(wv_banks[0], q_v, 0)
+        quantise_projection(wv_banks[1], q_v, 1)
 
-        m_new_ps = banks.tile([P, D], F32, name="m_new_ps", tag="ghn_ps")
-        for t in range(PACK):
-            nc.tensor.transpose(m_new_ps[:, chunk(t)], m_new[:, chunk(t)], ident[:])
         m_grouped = keep.tile([P, P * PACK], BF16, name="m_grouped", align_bytes=64)
         nc.scalar.copy(
             out=m_grouped[:].rearrange("q (s t) -> q s t", t=PACK),
@@ -239,8 +266,8 @@ def tile_instrumentspecificslotmemory_pb_s_kernel(
         m_scales = keep.tile([P, P], U8, name="m_scales", align_bytes=64)
         nc.vector.quantize_mx(out=m_codes[:].bitcast(FP8X4), scales=m_scales[:], in_=m_grouped[:])
 
-        def project(q_w, tag):
-            codes, scales = q_w
+        def project(tiles, tag):
+            grouped, codes, scales = tiles
             acc = banks.tile([P, D], F32, name="acc_" + tag, tag=tag)
             nc.tensor.matmul_mx(
                 out=acc[:],
@@ -253,8 +280,8 @@ def tile_instrumentspecificslotmemory_pb_s_kernel(
             )
             return acc
 
-        kt_ps = project(q_k, "gin_ps")
-        v_ps = project(q_v, "z_ps")
+        kt_ps = project(q_k, "a")
+        v_ps = project(q_v, "c")
         kt_sb = keep.tile([P, D], F32, name="kt_sb")
         v_sb = keep.tile([P, D], F32, name="v_sb")
         nc.scalar.copy(out=kt_sb[:], in_=kt_ps[:])

@@ -41,6 +41,11 @@ def tile_instrumentspecificslotmemory_pb_s_kernel(
         tpose = ctx.enter_context(tc.psum_pool(name="tpose", bufs=4))
         banks = ctx.enter_context(tc.psum_pool(name="banks", bufs=1))
 
+        idle_zeros = keep.tile([P, P * PACK], BF16, name="idle_zeros", align_bytes=64)
+        idle_codes = keep.tile([P, P], U32, name="idle_codes", align_bytes=64)
+        idle_scales = keep.tile([P, P], U8, name="idle_scales", align_bytes=64)
+        nc.vector.memset(idle_zeros[:], 0.0)
+        nc.vector.quantize_mx(out=idle_codes[:].bitcast(FP8X4), scales=idle_scales[:], in_=idle_zeros[:])
         ident = keep.tile([P, P], F32, name="ident")
         make_identity(nc, ident[:])
         bias_rows = keep.tile([P, 2 * P], BF16, name="bias_rows")
@@ -49,6 +54,21 @@ def tile_instrumentspecificslotmemory_pb_s_kernel(
         nc.vector.memset(zero[:], 0.0)
         minus_half = keep.tile([P, 1], F32, name="minus_half")
         nc.vector.memset(minus_half[:], -0.5)
+
+        def idle_passes(count, bank):
+            for i in range(count):
+                nc.tensor.matmul_mx(
+                    out=bank[:],
+                    lhsT=idle_codes[:].bitcast(FP8X4),
+                    lhsT_scale=idle_scales[:],
+                    rhs=idle_codes[:].bitcast(FP8X4),
+                    rhs_scale=idle_scales[:],
+                    start=True,
+                    stop=True,
+                )
+
+        idle_head = banks.tile([P, P], F32, name="idle_head", tag="d")
+        idle_passes(16, idle_head)
 
         act_sb = keep.tile([P, 2 * D], BF16, name="act_sb")
         nc.sync.dma_start(out=act_sb[:, 0:D], in_=agg.rearrange("b s d -> (b s) d"))
@@ -121,6 +141,7 @@ def tile_instrumentspecificslotmemory_pb_s_kernel(
         act_codes = keep.tile([P, 2 * P], U32, name="act_codes", align_bytes=64)
         act_scales = keep.tile([P, 2 * P], U8, name="act_scales", align_bytes=64)
         quantise(transpose(act_sb[:].bitcast(F32)), nc.vector.tensor_copy, act_grouped[:], act_codes[:], act_scales[:])
+        idle_passes(4, idle_head)
         m_t = act_grouped[:, MOLD * P * PACK : (MOLD + 1) * P * PACK].rearrange("q (s t) -> q t s", t=PACK)
 
         def gate_product(bank, first, chunks, terms):
@@ -143,7 +164,9 @@ def tile_instrumentspecificslotmemory_pb_s_kernel(
 
         for u in range(2):
             prepare(ih_r, q_ih_r, u, nc.scalar.copy)
+            idle_passes(4, idle_head)
             prepare(hh_r, q_hh_r, u, nc.scalar.copy)
+            idle_passes(4, idle_head)
 
         bias_ps = banks.tile([P, P], F32, name="bias_ps", tag="b")
         nc.tensor.transpose(bias_ps[:], bias_rows[:].bitcast(F32), ident[:])
@@ -155,6 +178,7 @@ def tile_instrumentspecificslotmemory_pb_s_kernel(
         nc.vector.tensor_tensor(out=bias_sum[:], in0=bias[:, 0, :, :], in1=bias[:, 1, :, :], op=ALU.add)
 
         prepare(ih_n, q_ih_n, 0, nc.scalar.copy)
+        idle_passes(4, idle_head)
         prepare(hh_n, q_hh_n, 0, nc.scalar.copy)
 
         r_ps = banks.tile([P, D], F32, name="r_ps", tag="a")
@@ -222,6 +246,8 @@ def tile_instrumentspecificslotmemory_pb_s_kernel(
             quantise(bank, nc.scalar.copy, grouped[:, u * HALF * PACK : (u + 1) * HALF * PACK], codes[:, half(u)], scales[:, half(u)])
 
         wv_banks = [transpose(wv_sb[:, u, :].bitcast(F32)) for u in range(2)]
+        idle_tail = banks.tile([P, P], F32, name="idle_tail", tag="a")
+        idle_passes(12, idle_tail)
 
         stats = keep.tile([P, 2, 6], F32, name="stats")
         nc.vector.bn_stats(out=stats[:, 0, :], in_=h_ps[0][:])
@@ -254,6 +280,7 @@ def tile_instrumentspecificslotmemory_pb_s_kernel(
             )
             for e in range(2):
                 nc.tensor.transpose(m_new_ps[:, chunk(2 * u + e)], m_new[:, chunk(2 * u + e)], ident[:])
+        idle_passes(12, idle_tail)
         quantise_projection(wv_banks[0], q_v, 0)
         quantise_projection(wv_banks[1], q_v, 1)
 

@@ -23,12 +23,8 @@ AGG, MOLD = 0, 1
 FLOPS = 2 * P * D * (2 * 3 * D + 2 * D)
 
 
-def chunk(t):
-    return slice(t * P, (t + 1) * P)
-
-
-def half(u):
-    return slice(u * HALF, (u + 1) * HALF)
+def chunks(first, count=1):
+    return slice(first * P, (first + count) * P)
 
 
 def tile_instrumentspecificslotmemory_pb_s_kernel(
@@ -41,65 +37,34 @@ def tile_instrumentspecificslotmemory_pb_s_kernel(
         tpose = ctx.enter_context(tc.psum_pool(name="tpose", bufs=4))
         banks = ctx.enter_context(tc.psum_pool(name="banks", bufs=1))
 
-        idle_zeros = keep.tile([P, P * PACK], BF16, name="idle_zeros", align_bytes=64)
-        idle_codes = keep.tile([P, P], U32, name="idle_codes", align_bytes=64)
-        idle_scales = keep.tile([P, P], U8, name="idle_scales", align_bytes=64)
-        nc.vector.memset(idle_zeros[:], 0.0)
-        nc.vector.quantize_mx(out=idle_codes[:].bitcast(FP8X4), scales=idle_scales[:], in_=idle_zeros[:])
         ident = keep.tile([P, P], F32, name="ident")
         make_identity(nc, ident[:])
         bias_rows = keep.tile([P, 2 * P], BF16, name="bias_rows")
         nc.vector.memset(bias_rows[:], 0.0)
-        zero = keep.tile([P, 1], F32, name="zero")
-        nc.vector.memset(zero[:], 0.0)
-        minus_half = keep.tile([P, 1], F32, name="minus_half")
-        nc.vector.memset(minus_half[:], -0.5)
-
-        def idle_passes(count, bank):
-            for i in range(count):
-                nc.tensor.matmul_mx(
-                    out=bank[:],
-                    lhsT=idle_codes[:].bitcast(FP8X4),
-                    lhsT_scale=idle_scales[:],
-                    rhs=idle_codes[:].bitcast(FP8X4),
-                    rhs_scale=idle_scales[:],
-                    start=True,
-                    stop=True,
-                )
-
-        idle_head = banks.tile([P, P], F32, name="idle_head", tag="d")
-        idle_passes(16, idle_head)
+        eps = keep.tile([P, 1], F32, name="eps")
+        nc.vector.memset(eps[:], EPS)
 
         act_sb = keep.tile([P, 2 * D], BF16, name="act_sb")
         nc.sync.dma_start(out=act_sb[:, 0:D], in_=agg.rearrange("b s d -> (b s) d"))
         nc.sync.dma_start(out=act_sb[:, D : 2 * D], in_=M_old.rearrange("b s d -> (b s) d"))
 
-        def load_gate(w, gate, name):
-            rows = keep.tile([P, 2, 2 * D], BF16, name=name)
-            for u in range(2):
+        ih = [keep.tile([P, PACK * D], BF16, name="ih%d" % gate) for gate in range(3)]
+        hh = [keep.tile([P, PACK * D], BF16, name="hh%d" % gate) for gate in range(3)]
+        for gate, u in ((R, 0), (N, 0), (R, 1), (N, 1), (Z, 0), (Z, 1)):
+            for rows, w in ((ih[gate], W_ih), (hh[gate], W_hh)):
                 first = gate * D + u * HALF
                 nc.sync.dma_start(
-                    out=rows[:, u, :], in_=w[first : first + HALF, :].rearrange("(p e) k -> p (e k)", e=2)
+                    out=rows[:, u * 2 * D : (u + 1) * 2 * D],
+                    in_=w[first : first + HALF, :].rearrange("(p e) k -> p (e k)", e=2),
                 )
-            return rows
-
-        def load_projection(w, name):
-            rows = keep.tile([P, 2, 2 * D], BF16, name=name)
+        wk_sb = keep.tile([P, PACK * D], BF16, name="wk_sb")
+        wv_sb = keep.tile([P, PACK * D], BF16, name="wv_sb")
+        for rows, w in ((wk_sb, Wk), (wv_sb, Wv)):
             for u in range(2):
                 nc.sync.dma_start(
-                    out=rows[:, u, :].rearrange("p (c k) -> p c k", c=2),
+                    out=rows[:, u * 2 * D : (u + 1) * 2 * D].rearrange("p (c k) -> p c k", c=2),
                     in_=w[u * HALF : (u + 1) * HALF, :].rearrange("(c p) k -> p c k", p=P),
                 )
-            return rows
-
-        ih_r = load_gate(W_ih, R, "ih_r")
-        hh_r = load_gate(W_hh, R, "hh_r")
-        ih_n = load_gate(W_ih, N, "ih_n")
-        hh_n = load_gate(W_hh, N, "hh_n")
-        ih_z = load_gate(W_ih, Z, "ih_z")
-        hh_z = load_gate(W_hh, Z, "hh_z")
-        wk_sb = load_projection(Wk, "wk_sb")
-        wv_sb = load_projection(Wv, "wv_sb")
         gain = keep.tile([P, D], BF16, name="gain")
         shift = keep.tile([P, D], BF16, name="shift")
         nc.sync.dma_start(out=gain[:], in_=g_mem.partition_broadcast(P))
@@ -107,211 +72,218 @@ def tile_instrumentspecificslotmemory_pb_s_kernel(
 
         nc.scalar.dma_start(out=bias_rows[0:6, :], in_=b_ih.rearrange("(j x) -> j x", x=2 * P))
         nc.scalar.dma_start(out=bias_rows[6:12, :], in_=b_hh.rearrange("(j x) -> j x", x=2 * P))
-        table_warm = keep.tile([P, 1], F32, name="table_warm")
-        nc.scalar.activation(out=table_warm[:], in_=zero[:], func=ACT.Sigmoid)
+        table_warm = keep.tile([P, 2], F32, name="table_warm")
+        nc.scalar.activation(out=table_warm[:, 0:1], in_=eps[:], func=ACT.Sigmoid)
 
-        def transpose(words):
-            bank = tpose.tile([P, 2 * 2 * P], F32, name="tp")
-            for c in range(2):
+        def transpose(rows, first, count):
+            words = rows[:].bitcast(F32)
+            bank = tpose.tile([P, count * 2 * P], F32, name="tp")
+            for c in range(count):
                 for u in range(2):
-                    nc.tensor.transpose(
-                        bank[:, chunk(2 * c + u)], words[:, c * WORDS + u * P : c * WORDS + (u + 1) * P], ident[:]
-                    )
+                    start = (first + c) * WORDS + u * P
+                    nc.tensor.transpose(bank[:, chunks(2 * c + u)], words[:, start : start + P], ident[:])
             return bank
 
-        def quantise(bank, copy, grouped, codes, scales):
+        def copy_out(bank, tiles, first, count, copy):
+            grouped, codes, scales = tiles
             copy(
-                out=grouped.bitcast(F32).rearrange("q (c r u) -> q c r u", c=2, u=2),
-                in_=bank[:].rearrange("q (c u r) -> q c r u", c=2, u=2),
+                out=grouped[:, chunks(first * PACK, count * PACK)].bitcast(F32).rearrange("q (c r u) -> q c r u", c=count, u=2),
+                in_=bank[:].rearrange("q (c u r) -> q c r u", c=count, u=2),
             )
-            nc.vector.quantize_mx(out=codes.bitcast(FP8X4), scales=scales, in_=grouped)
 
-        def operand(name):
-            grouped = keep.tile([P, D * PACK], BF16, name=name + "_grouped", align_bytes=64)
-            codes = keep.tile([P, D], U32, name=name + "_codes", align_bytes=64)
-            scales = keep.tile([P, D], U8, name=name + "_scales", align_bytes=64)
+        def quantise(tiles, first, count):
+            grouped, codes, scales = tiles
+            nc.vector.quantize_mx(
+                out=codes[:, chunks(first, count)].bitcast(FP8X4),
+                scales=scales[:, chunks(first, count)],
+                in_=grouped[:, chunks(first * PACK, count * PACK)],
+            )
+
+        def prepare(rows, tiles, first, count, copy):
+            copy_out(transpose(rows, first, count), tiles, first, count, copy)
+            quantise(tiles, first, count)
+
+        def operand(name, count):
+            grouped = keep.tile([P, count * P * PACK], BF16, name=name + "_grouped", align_bytes=64)
+            codes = keep.tile([P, count * P], U32, name=name + "_codes", align_bytes=64)
+            scales = keep.tile([P, count * P], U8, name=name + "_scales", align_bytes=64)
             return grouped, codes, scales
 
-        def prepare(rows, tiles, u, copy):
-            grouped, codes, scales = tiles
-            bank = transpose(rows[:, u, :].bitcast(F32))
-            quantise(bank, copy, grouped[:, u * HALF * PACK : (u + 1) * HALF * PACK], codes[:, half(u)], scales[:, half(u)])
+        q_act = operand("act", 2)
+        q_ih = [operand("q_ih%d" % gate, PACK) for gate in range(3)]
+        q_hh = [operand("q_hh%d" % gate, PACK) for gate in range(3)]
+        q_k, q_v = operand("wk", PACK), operand("wv", PACK)
+        q_m = operand("m_new", 1)
 
-        act_grouped = keep.tile([P, 2 * P * PACK], BF16, name="act_grouped", align_bytes=64)
-        act_codes = keep.tile([P, 2 * P], U32, name="act_codes", align_bytes=64)
-        act_scales = keep.tile([P, 2 * P], U8, name="act_scales", align_bytes=64)
-        quantise(transpose(act_sb[:].bitcast(F32)), nc.vector.tensor_copy, act_grouped[:], act_codes[:], act_scales[:])
-        idle_passes(4, idle_head)
-        m_t = act_grouped[:, MOLD * P * PACK : (MOLD + 1) * P * PACK].rearrange("q (s t) -> q t s", t=PACK)
-
-        def gate_product(bank, first, chunks, terms):
-            for t in chunks:
+        def gate_product(bank, base, first, count, terms):
+            for t in range(first, first + count):
                 for i, ((grouped, codes, scales), a) in enumerate(terms):
                     nc.tensor.matmul_mx(
-                        out=bank[:, chunk(t - first)],
-                        lhsT=codes[:, chunk(t)].bitcast(FP8X4),
-                        lhsT_scale=scales[:, chunk(t)],
-                        rhs=act_codes[:, chunk(a)].bitcast(FP8X4),
-                        rhs_scale=act_scales[:, chunk(a)],
+                        out=bank[:, chunks(t - base)],
+                        lhsT=codes[:, chunks(t)].bitcast(FP8X4),
+                        lhsT_scale=scales[:, chunks(t)],
+                        rhs=q_act[1][:, chunks(a)].bitcast(FP8X4),
+                        rhs_scale=q_act[2][:, chunks(a)],
                         start=(i == 0),
                         stop=(i == len(terms) - 1),
                     )
 
-        q_ih_r, q_hh_r = operand("ih_r"), operand("hh_r")
-        q_ih_n, q_hh_n = operand("ih_n"), operand("hh_n")
-        q_ih_z, q_hh_z = operand("ih_z"), operand("hh_z")
-        q_k, q_v = operand("wk"), operand("wv")
+        def squash(out, pre, base, first, count, func, bias):
+            for t in range(first, first + count):
+                nc.scalar.activation(out=out[:, chunks(t)], in_=pre[:, chunks(t - base)], func=func, bias=bias[:, t : t + 1])
 
-        for u in range(2):
-            prepare(ih_r, q_ih_r, u, nc.scalar.copy)
-            idle_passes(4, idle_head)
-            prepare(hh_r, q_hh_r, u, nc.scalar.copy)
-            idle_passes(4, idle_head)
+        r_ps = banks.tile([P, D], F32, name="r_ps", tag="a")
+        gin_ps = banks.tile([P, D], F32, name="gin_ps", tag="c")
+        ghn_ps = banks.tile([P, D], F32, name="ghn_ps", tag="d")
+        bias = keep.tile([P, 2, 3, PACK], F32, name="bias")
+        bias_sum = keep.tile([P, 3, PACK], F32, name="bias_sum")
+        r = keep.tile([P, D], F32, name="r")
+        n_pre = keep.tile([P, D], F32, name="n_pre")
+        n = keep.tile([P, D], F32, name="n")
+        z = keep.tile([P, D], F32, name="z")
+        h = keep.tile([P, D], F32, name="h")
+        m_t = q_act[0][:, chunks(MOLD * PACK, PACK)].rearrange("q (s t) -> q t s", t=PACK)
+
+        def r_gate(u):
+            gate_product(r_ps, 0, 2 * u, 2, [(q_ih[R], AGG), (q_hh[R], MOLD)])
+            squash(r, r_ps, 0, 2 * u, 2, ACT.Sigmoid, bias_sum[:, R, :])
+
+        def n_products(u):
+            gate_product(ghn_ps, 0, 2 * u, 2, [(q_hh[N], MOLD)])
+            gate_product(gin_ps, 0, 2 * u, 2, [(q_ih[N], AGG)])
+            for t in (2 * u, 2 * u + 1):
+                nc.vector.scalar_tensor_tensor(
+                    out=n_pre[:, chunks(t)], in0=ghn_ps[:, chunks(t)], scalar=bias[:, 1, N, t : t + 1], in1=r[:, chunks(t)],
+                    op0=ALU.add, op1=ALU.mult,
+                )
+
+        def n_sum(u):
+            cols = chunks(2 * u, 2)
+            nc.vector.tensor_tensor(out=n_pre[:, cols], in0=gin_ps[:, cols], in1=n_pre[:, cols], op=ALU.add)
+
+        def n_gate(u):
+            squash(n, n_pre, 0, 2 * u, 2, ACT.Tanh, bias[:, 0, N, :])
+            cols = chunks(2 * u, 2)
+            nc.vector.tensor_tensor(
+                out=h[:, cols].rearrange("q (t s) -> q t s", t=2), in0=m_t[:, 2 * u : 2 * u + 2, :],
+                in1=n[:, cols].rearrange("q (t s) -> q t s", t=2), op=ALU.subtract,
+            )
+
+        prepare(act_sb, q_act, 0, 2, nc.vector.tensor_copy)
+        prepare(ih[R], q_ih[R], 0, 2, nc.scalar.copy)
+        prepare(hh[R], q_hh[R], 0, 2, nc.scalar.copy)
 
         bias_ps = banks.tile([P, P], F32, name="bias_ps", tag="b")
         nc.tensor.transpose(bias_ps[:], bias_rows[:].bitcast(F32), ident[:])
-        bias = keep.tile([P, 2, 3, PACK], F32, name="bias")
         nc.vector.tensor_copy(
             out=bias[:].rearrange("q a g t -> q (a g t)"), in_=bias_ps[:].bitcast(BF16)[:, 0 : 2 * 3 * PACK]
         )
-        bias_sum = keep.tile([P, 3, PACK], F32, name="bias_sum")
         nc.vector.tensor_tensor(out=bias_sum[:], in0=bias[:, 0, :, :], in1=bias[:, 1, :, :], op=ALU.add)
 
-        prepare(ih_n, q_ih_n, 0, nc.scalar.copy)
-        idle_passes(4, idle_head)
-        prepare(hh_n, q_hh_n, 0, nc.scalar.copy)
+        prepare(ih[N], q_ih[N], 0, 2, nc.scalar.copy)
+        prepare(hh[N], q_hh[N], 0, 2, nc.scalar.copy)
+        prepare(ih[R], q_ih[R], 2, 2, nc.scalar.copy)
+        r_gate(0)
+        copy_out(transpose(hh[R], 2, 2), q_hh[R], 2, 2, nc.scalar.copy)
+        n_products(0)
+        quantise(q_hh[R], 2, 2)
+        n_sum(0)
+        prepare(ih[N], q_ih[N], 2, 2, nc.scalar.copy)
+        prepare(hh[N], q_hh[N], 2, 2, nc.scalar.copy)
+        n_gate(0)
+        prepare(ih[Z], q_ih[Z], 0, 2, nc.scalar.copy)
+        r_gate(1)
+        copy_out(transpose(hh[Z], 0, 2), q_hh[Z], 0, 2, nc.scalar.copy)
+        copy_out(transpose(ih[Z], 2, 2), q_ih[Z], 2, 2, nc.scalar.copy)
+        n_products(1)
+        quantise(q_hh[Z], 0, 2)
+        n_sum(1)
+        quantise(q_ih[Z], 2, 2)
+        prepare(hh[Z], q_hh[Z], 2, 1, nc.scalar.copy)
+        prepare(hh[Z], q_hh[Z], 3, 1, nc.scalar.copy)
+        pieces = ((0, 2), (2, 1), (3, 1))
+        squash(n, n_pre, 0, 2, 2, ACT.Tanh, bias[:, 0, N, :])
 
-        r_ps = banks.tile([P, D], F32, name="r_ps", tag="a")
-        gate_product(r_ps, 0, range(PACK), [(q_ih_r, AGG), (q_hh_r, MOLD)])
-        r = keep.tile([P, D], F32, name="r")
-        for t in range(PACK):
-            nc.scalar.activation(
-                out=r[:, chunk(t)], in_=r_ps[:, chunk(t)], func=ACT.Sigmoid, bias=bias_sum[:, R, t : t + 1]
-            )
+        wk_banks = [transpose(wk_sb, 0, 2)]
+        for (first, count), tag in zip(pieces, ("b", "a", "c")):
+            z_ps = banks.tile([P, count * P], F32, name="z_ps", tag=tag)
+            gate_product(z_ps, first, first, count, [(q_ih[Z], AGG), (q_hh[Z], MOLD)])
+            squash(z, z_ps, first, first, count, ACT.Sigmoid, bias_sum[:, Z, :])
+        nc.scalar.activation(out=table_warm[:, 1:2], in_=eps[:], func=ACT.Abs_reciprocal_sqrt)
+        nc.vector.tensor_tensor(
+            out=h[:, chunks(2, 2)].rearrange("q (t s) -> q t s", t=2), in0=m_t[:, 2:4, :],
+            in1=n[:, chunks(2, 2)].rearrange("q (t s) -> q t s", t=2), op=ALU.subtract,
+        )
+        wk_banks.append(transpose(wk_sb, 2, 2))
+        wv_banks = [transpose(wv_sb, 0, 2)]
 
-        prepare(ih_n, q_ih_n, 1, nc.scalar.copy)
-        prepare(hh_n, q_hh_n, 1, nc.scalar.copy)
-        prepare(ih_z, q_ih_z, 0, nc.scalar.copy)
-        prepare(hh_z, q_hh_z, 0, nc.scalar.copy)
-
-        gin_ps = banks.tile([P, D], F32, name="gin_ps", tag="c")
-        ghn_ps = banks.tile([P, D], F32, name="ghn_ps", tag="d")
-        gate_product(ghn_ps, 0, range(PACK), [(q_hh_n, MOLD)])
-        gate_product(gin_ps, 0, range(PACK), [(q_ih_n, AGG)])
-        n_pre = keep.tile([P, D], F32, name="n_pre")
-        for t in range(PACK):
-            nc.vector.scalar_tensor_tensor(
-                out=n_pre[:, chunk(t)], in0=ghn_ps[:, chunk(t)], scalar=bias[:, 1, N, t : t + 1], in1=r[:, chunk(t)],
-                op0=ALU.add, op1=ALU.mult,
-            )
-        nc.vector.tensor_tensor(out=n_pre[:], in0=gin_ps[:], in1=n_pre[:], op=ALU.add)
-
-        prepare(ih_z, q_ih_z, 1, nc.scalar.copy)
-        prepare(hh_z, q_hh_z, 1, nc.vector.tensor_copy)
-
-        n = keep.tile([P, D], F32, name="n")
-        for t in range(PACK):
-            nc.scalar.activation(
-                out=n[:, chunk(t)], in_=n_pre[:, chunk(t)], func=ACT.Tanh, bias=bias[:, 0, N, t : t + 1]
-            )
-
-        z = keep.tile([P, D], F32, name="z")
-        wk_banks = []
-        for u, tag in ((0, "b"), (1, "a")):
-            wk_banks.append(transpose(wk_sb[:, u, :].bitcast(F32)))
-            z_ps = banks.tile([P, HALF], F32, name="z_ps", tag=tag)
-            gate_product(z_ps, 2 * u, (2 * u, 2 * u + 1), [(q_ih_z, AGG), (q_hh_z, MOLD)])
-            for t in (2 * u, 2 * u + 1):
-                nc.scalar.activation(
-                    out=z[:, chunk(t)], in_=z_ps[:, chunk(t - 2 * u)], func=ACT.Sigmoid, bias=bias_sum[:, Z, t : t + 1]
-                )
-            if u == 0:
-                m_minus_n = keep.tile([P, D], F32, name="m_minus_n")
-                nc.vector.tensor_tensor(
-                    out=m_minus_n[:].rearrange("q (t s) -> q t s", t=PACK), in0=m_t,
-                    in1=n[:].rearrange("q (t s) -> q t s", t=PACK), op=ALU.subtract,
-                )
-
-        h = keep.tile([P, D], F32, name="h")
         h_ps = []
-        for u, tag in ((0, "c"), (1, "d")):
-            nc.vector.tensor_tensor(out=h[:, half(u)], in0=z[:, half(u)], in1=m_minus_n[:, half(u)], op=ALU.mult)
-            nc.vector.tensor_tensor(out=h[:, half(u)], in0=h[:, half(u)], in1=n[:, half(u)], op=ALU.add)
-            h_ps.append(banks.tile([P, HALF], F32, name="h_ps", tag=tag))
-            for e in range(2):
-                nc.tensor.transpose(h_ps[u][:, chunk(e)], h[:, chunk(2 * u + e)], ident[:])
+        for (first, count), tag in zip(pieces, ("d", "b", "a")):
+            cols = chunks(first, count)
+            nc.vector.tensor_tensor(out=h[:, cols], in0=z[:, cols], in1=h[:, cols], op=ALU.mult)
+            nc.vector.tensor_tensor(out=h[:, cols], in0=h[:, cols], in1=n[:, cols], op=ALU.add)
+            h_ps.append(banks.tile([P, count * P], F32, name="h_ps", tag=tag))
+            for c in range(count):
+                nc.tensor.transpose(h_ps[-1][:, chunks(c)], h[:, chunks(first + c)], ident[:])
+        wv_banks.append(transpose(wv_sb, 2, 2))
 
-        def quantise_projection(bank, tiles, u):
-            grouped, codes, scales = tiles
-            quantise(bank, nc.scalar.copy, grouped[:, u * HALF * PACK : (u + 1) * HALF * PACK], codes[:, half(u)], scales[:, half(u)])
+        def spread(vector, first, count):
+            u, e = first // 2, first % 2
+            return vector[:, u * HALF : (u + 1) * HALF].rearrange("s (q e) -> s e q", e=2)[:, e : e + count, :]
 
-        wv_banks = [transpose(wv_sb[:, u, :].bitcast(F32)) for u in range(2)]
-        idle_tail = banks.tile([P, P], F32, name="idle_tail", tag="a")
-        idle_passes(12, idle_tail)
-
-        stats = keep.tile([P, 2, 6], F32, name="stats")
-        nc.vector.bn_stats(out=stats[:, 0, :], in_=h_ps[0][:])
-        quantise_projection(wk_banks[0], q_k, 0)
-        nc.vector.bn_stats(out=stats[:, 1, :], in_=h_ps[1][:])
+        copy_out(wk_banks[0], q_k, 0, 2, nc.scalar.copy)
+        stats = keep.tile([P, len(pieces), 6], F32, name="stats")
+        for i in range(len(pieces)):
+            nc.vector.bn_stats(out=stats[:, i, :], in_=h_ps[i][:])
         mean_var = keep.tile([P, 2], F32, name="mean_var")
-        nc.vector.bn_aggr(out=mean_var[:], in_=stats[:].rearrange("s u x -> s (u x)"))
-        var_eps = keep.tile([P, 1], F32, name="var_eps")
-        nc.vector.tensor_scalar_add(out=var_eps[:], in0=mean_var[:, 1:2], scalar1=EPS)
+        nc.vector.bn_aggr(out=mean_var[:], in_=stats[:].rearrange("s i x -> s (i x)"))
         rstd = keep.tile([P, 1], F32, name="rstd")
-        nc.gpsimd.tensor_tensor(out=rstd[:], in0=var_eps[:], in1=minus_half[:], op=ALU.pow)
+        nc.scalar.activation(out=rstd[:], in_=mean_var[:, 1:2], func=ACT.Abs_reciprocal_sqrt, bias=eps[:, 0:1])
+        copy_out(wk_banks[1], q_k, 2, 2, nc.scalar.copy)
+        copy_out(wv_banks[0], q_v, 0, 2, nc.scalar.copy)
+        copy_out(wv_banks[1], q_v, 2, 2, nc.scalar.copy)
         m_new = keep.tile([P, D], F32, name="m_new")
-        for u in range(2):
+        for i, (first, count) in enumerate(pieces):
             nc.vector.scalar_tensor_tensor(
-                out=m_new[:, half(u)].rearrange("s (e q) -> s e q", e=2),
-                in0=h_ps[u][:].rearrange("s (e q) -> s e q", e=2),
+                out=m_new[:, chunks(first, count)].rearrange("s (t q) -> s t q", t=count),
+                in0=h_ps[i][:].rearrange("s (t q) -> s t q", t=count),
                 scalar=mean_var[:, 0:1],
-                in1=gain[:, half(u)].rearrange("s (q e) -> s e q", e=2),
+                in1=spread(gain, first, count),
                 op0=ALU.subtract, op1=ALU.mult,
             )
-        quantise_projection(wk_banks[1], q_k, 1)
-        m_new_ps = banks.tile([P, D], F32, name="m_new_ps", tag="b")
-        for u in range(2):
+        m_new_ps = banks.tile([P, D], F32, name="m_new_ps", tag="c")
+        for first in (0, 2):
             nc.vector.scalar_tensor_tensor(
-                out=m_new[:, half(u)].rearrange("s (e q) -> s e q", e=2),
-                in0=m_new[:, half(u)].rearrange("s (e q) -> s e q", e=2),
+                out=m_new[:, chunks(first, 2)].rearrange("s (t q) -> s t q", t=2),
+                in0=m_new[:, chunks(first, 2)].rearrange("s (t q) -> s t q", t=2),
                 scalar=rstd[:, 0:1],
-                in1=shift[:, half(u)].rearrange("s (q e) -> s e q", e=2),
+                in1=spread(shift, first, 2),
                 op0=ALU.mult, op1=ALU.add,
             )
-            for e in range(2):
-                nc.tensor.transpose(m_new_ps[:, chunk(2 * u + e)], m_new[:, chunk(2 * u + e)], ident[:])
-        idle_passes(12, idle_tail)
-        quantise_projection(wv_banks[0], q_v, 0)
-        quantise_projection(wv_banks[1], q_v, 1)
+            for t in (first, first + 1):
+                nc.tensor.transpose(m_new_ps[:, chunks(t)], m_new[:, chunks(t)], ident[:])
+        for tiles in (q_k, q_v):
+            for first in (0, 2):
+                quantise(tiles, first, 2)
 
-        m_grouped = keep.tile([P, P * PACK], BF16, name="m_grouped", align_bytes=64)
         nc.scalar.copy(
-            out=m_grouped[:].rearrange("q (s t) -> q s t", t=PACK),
+            out=q_m[0][:].rearrange("q (s t) -> q s t", t=PACK),
             in_=m_new_ps[:].rearrange("q (t s) -> q s t", t=PACK),
         )
-        m_codes = keep.tile([P, P], U32, name="m_codes", align_bytes=64)
-        m_scales = keep.tile([P, P], U8, name="m_scales", align_bytes=64)
-        nc.vector.quantize_mx(out=m_codes[:].bitcast(FP8X4), scales=m_scales[:], in_=m_grouped[:])
+        quantise(q_m, 0, 1)
 
-        def project(tiles, tag):
-            grouped, codes, scales = tiles
-            acc = banks.tile([P, D], F32, name="acc_" + tag, tag=tag)
-            nc.tensor.matmul_mx(
-                out=acc[:],
-                lhsT=m_codes[:].bitcast(FP8X4),
-                lhsT_scale=m_scales[:],
-                rhs=codes[:].bitcast(FP8X4),
-                rhs_scale=scales[:],
-                start=True,
-                stop=True,
-            )
-            return acc
-
-        kt_ps = project(q_k, "a")
-        v_ps = project(q_v, "c")
-        kt_sb = keep.tile([P, D], F32, name="kt_sb")
-        v_sb = keep.tile([P, D], F32, name="v_sb")
-        nc.scalar.copy(out=kt_sb[:], in_=kt_ps[:])
-        nc.vector.tensor_copy(out=v_sb[:], in_=v_ps[:])
-        nc.sync.dma_start(out=out_0.rearrange("b s d -> (b s) d"), in_=kt_sb[:])
-        nc.scalar.dma_start(out=out_1.rearrange("b s d -> (b s) d"), in_=v_sb[:])
+        for name, (grouped, codes, scales), out in (("kt", q_k, out_0), ("v", q_v, out_1)):
+            result = keep.tile([P, D], F32, name=name)
+            for u, copy in ((0, nc.scalar.copy), (1, nc.vector.tensor_copy)):
+                acc = tpose.tile([P, HALF], F32, name="tp")
+                nc.tensor.matmul_mx(
+                    out=acc[:],
+                    lhsT=q_m[1][:].bitcast(FP8X4),
+                    lhsT_scale=q_m[2][:],
+                    rhs=codes[:, chunks(2 * u, 2)].bitcast(FP8X4),
+                    rhs_scale=scales[:, chunks(2 * u, 2)],
+                    start=True,
+                    stop=True,
+                )
+                copy(out=result[:, chunks(2 * u, 2)], in_=acc[:])
+            nc.sync.dma_start(out=out.rearrange("b s d -> (b s) d"), in_=result[:])

@@ -43,6 +43,8 @@ def tile_instrumentspecificslotmemory_pb_s_kernel(
         nc.vector.memset(bias_rows[:], 0.0)
         eps = keep.tile([P, 1], F32, name="eps")
         nc.vector.memset(eps[:], EPS)
+        zeros = keep.tile([P, P], F32, name="zeros")
+        nc.vector.memset(zeros[:], 0.0)
 
         act_sb = keep.tile([P, 2 * D], BF16, name="act_sb")
         nc.sync.dma_start(out=act_sb[:, 0:D], in_=agg.rearrange("b s d -> (b s) d"))
@@ -169,6 +171,12 @@ def tile_instrumentspecificslotmemory_pb_s_kernel(
                 in1=n[:, cols].rearrange("q (t s) -> q t s", t=2), op=ALU.subtract,
             )
 
+        def keep_clock(count):
+            idle_ps = banks.tile([P, P], F32, name="idle_ps", tag="b")
+            for i in range(count):
+                nc.tensor.matmul(idle_ps[:], zeros[:], zeros[:], start=True, stop=True)
+
+        keep_clock(5)
         prepare(act_sb, q_act, 0, 2, nc.vector.tensor_copy)
         prepare(ih[R], q_ih[R], 0, 2, nc.scalar.copy)
         prepare(hh[R], q_hh[R], 0, 2, nc.scalar.copy)
@@ -183,8 +191,10 @@ def tile_instrumentspecificslotmemory_pb_s_kernel(
         prepare(ih[N], q_ih[N], 0, 2, nc.scalar.copy)
         prepare(hh[N], q_hh[N], 0, 2, nc.scalar.copy)
         prepare(ih[R], q_ih[R], 2, 2, nc.scalar.copy)
+        keep_clock(1)
         r_gate(0)
         copy_out(transpose(hh[R], 2, 2), q_hh[R], 2, 2, nc.scalar.copy)
+        keep_clock(1)
         n_products(0)
         quantise(q_hh[R], 2, 2)
         n_sum(0)
@@ -192,9 +202,11 @@ def tile_instrumentspecificslotmemory_pb_s_kernel(
         prepare(hh[N], q_hh[N], 2, 2, nc.scalar.copy)
         n_gate(0)
         prepare(ih[Z], q_ih[Z], 0, 2, nc.scalar.copy)
+        keep_clock(1)
         r_gate(1)
         copy_out(transpose(hh[Z], 0, 2), q_hh[Z], 0, 2, nc.scalar.copy)
         copy_out(transpose(ih[Z], 2, 2), q_ih[Z], 2, 2, nc.scalar.copy)
+        keep_clock(1)
         n_products(1)
         quantise(q_hh[Z], 0, 2)
         n_sum(1)
@@ -242,34 +254,31 @@ def tile_instrumentspecificslotmemory_pb_s_kernel(
         copy_out(wk_banks[1], q_k, 2, 2, nc.scalar.copy)
         copy_out(wv_banks[0], q_v, 0, 2, nc.scalar.copy)
         copy_out(wv_banks[1], q_v, 2, 2, nc.scalar.copy)
-        m_new = keep.tile([P, D], F32, name="m_new")
+        centred = keep.tile([P, D], F32, name="centred")
         for i, (first, count) in enumerate(pieces):
             nc.vector.scalar_tensor_tensor(
-                out=m_new[:, chunks(first, count)].rearrange("s (t q) -> s t q", t=count),
+                out=centred[:, chunks(first, count)].rearrange("s (t q) -> s t q", t=count),
                 in0=h_ps[i][:].rearrange("s (t q) -> s t q", t=count),
                 scalar=mean_var[:, 0:1],
                 in1=spread(gain, first, count),
                 op0=ALU.subtract, op1=ALU.mult,
             )
-        m_new_ps = banks.tile([P, D], F32, name="m_new_ps", tag="c")
-        for first in (0, 2):
+        m_new = keep.tile([P, D], BF16, name="m_new")
+        m_bank = banks.tile([P, 2 * P], F32, name="m_bank", tag="c")
+        for u in range(2):
+            half = slice(u * HALF, (u + 1) * HALF)
             nc.vector.scalar_tensor_tensor(
-                out=m_new[:, chunks(first, 2)].rearrange("s (t q) -> s t q", t=2),
-                in0=m_new[:, chunks(first, 2)].rearrange("s (t q) -> s t q", t=2),
+                out=m_new[:, half].rearrange("s (q e) -> s q e", e=2),
+                in0=centred[:, chunks(2 * u, 2)].rearrange("s (e q) -> s q e", e=2),
                 scalar=rstd[:, 0:1],
-                in1=spread(shift, first, 2),
+                in1=shift[:, half].rearrange("s (q e) -> s q e", e=2),
                 op0=ALU.mult, op1=ALU.add,
             )
-            for t in (first, first + 1):
-                nc.tensor.transpose(m_new_ps[:, chunks(t)], m_new[:, chunks(t)], ident[:])
+            nc.tensor.transpose(m_bank[:, chunks(u)], m_new[:].bitcast(F32)[:, chunks(u)], ident[:])
         for tiles in (q_k, q_v):
             for first in (0, 2):
                 quantise(tiles, first, 2)
-
-        nc.scalar.copy(
-            out=q_m[0][:].rearrange("q (s t) -> q s t", t=PACK),
-            in_=m_new_ps[:].rearrange("q (t s) -> q s t", t=PACK),
-        )
+        copy_out(m_bank, q_m, 0, 1, nc.scalar.copy)
         quantise(q_m, 0, 1)
 
         for name, (grouped, codes, scales), out in (("kt", q_k, out_0), ("v", q_v, out_1)):

@@ -64,8 +64,8 @@ def tile_instrumentspecificslotmemory_pb_s_kernel(
         for rows, w in ((wk_sb, Wk), (wv_sb, Wv)):
             for u in range(2):
                 nc.sync.dma_start(
-                    out=rows[:, u * 2 * D : (u + 1) * 2 * D].rearrange("p (c k) -> p c k", c=2),
-                    in_=w[u * HALF : (u + 1) * HALF, :].rearrange("(c p) k -> p c k", p=P),
+                    out=rows[:, u * 2 * D : (u + 1) * 2 * D],
+                    in_=w[u * HALF : (u + 1) * HALF, :].rearrange("(p e) k -> p (e k)", e=2),
                 )
         gain = keep.tile([P, D], BF16, name="gain")
         shift = keep.tile([P, D], BF16, name="shift")
@@ -191,10 +191,8 @@ def tile_instrumentspecificslotmemory_pb_s_kernel(
         prepare(ih[N], q_ih[N], 0, 2, nc.scalar.copy)
         prepare(hh[N], q_hh[N], 0, 2, nc.scalar.copy)
         prepare(ih[R], q_ih[R], 2, 2, nc.scalar.copy)
-        keep_clock(1)
         r_gate(0)
         copy_out(transpose(hh[R], 2, 2), q_hh[R], 2, 2, nc.scalar.copy)
-        keep_clock(1)
         n_products(0)
         quantise(q_hh[R], 2, 2)
         n_sum(0)
@@ -202,11 +200,9 @@ def tile_instrumentspecificslotmemory_pb_s_kernel(
         prepare(hh[N], q_hh[N], 2, 2, nc.scalar.copy)
         n_gate(0)
         prepare(ih[Z], q_ih[Z], 0, 2, nc.scalar.copy)
-        keep_clock(1)
         r_gate(1)
         copy_out(transpose(hh[Z], 0, 2), q_hh[Z], 0, 2, nc.scalar.copy)
         copy_out(transpose(ih[Z], 2, 2), q_ih[Z], 2, 2, nc.scalar.copy)
-        keep_clock(1)
         n_products(1)
         quantise(q_hh[Z], 0, 2)
         n_sum(1)
@@ -230,13 +226,24 @@ def tile_instrumentspecificslotmemory_pb_s_kernel(
         wv_banks = [transpose(wv_sb, 0, 2)]
 
         h_ps = []
-        for (first, count), tag in zip(pieces, ("d", "b", "a")):
+        def scaled(first, count):
             cols = chunks(first, count)
             nc.vector.tensor_tensor(out=h[:, cols], in0=z[:, cols], in1=h[:, cols], op=ALU.mult)
+
+        def blended(first, count, tag):
+            cols = chunks(first, count)
             nc.vector.tensor_tensor(out=h[:, cols], in0=h[:, cols], in1=n[:, cols], op=ALU.add)
-            h_ps.append(banks.tile([P, count * P], F32, name="h_ps", tag=tag))
+            bank = banks.tile([P, count * P], F32, name="h_ps", tag=tag)
             for c in range(count):
-                nc.tensor.transpose(h_ps[-1][:, chunks(c)], h[:, chunks(first + c)], ident[:])
+                nc.tensor.transpose(bank[:, chunks(c)], h[:, chunks(first + c)], ident[:])
+            h_ps.append(bank)
+
+        scaled(0, 2)
+        blended(0, 2, "d")
+        scaled(2, 1)
+        scaled(3, 1)
+        blended(2, 1, "b")
+        blended(3, 1, "a")
         wv_banks.append(transpose(wv_sb, 2, 2))
 
         def spread(vector, first, count):
@@ -283,7 +290,9 @@ def tile_instrumentspecificslotmemory_pb_s_kernel(
 
         for name, (grouped, codes, scales), out in (("kt", q_k, out_0), ("v", q_v, out_1)):
             result = keep.tile([P, D], F32, name=name)
+            rows_out = out.rearrange("b s d -> (b s) d")
             for u, copy in ((0, nc.scalar.copy), (1, nc.vector.tensor_copy)):
+                half = slice(u * HALF, (u + 1) * HALF)
                 acc = tpose.tile([P, HALF], F32, name="tp")
                 nc.tensor.matmul_mx(
                     out=acc[:],
@@ -294,5 +303,8 @@ def tile_instrumentspecificslotmemory_pb_s_kernel(
                     start=True,
                     stop=True,
                 )
-                copy(out=result[:, chunks(2 * u, 2)], in_=acc[:])
-            nc.sync.dma_start(out=out.rearrange("b s d -> (b s) d"), in_=result[:])
+                copy(
+                    out=result[:, half].rearrange("s (q e) -> s q e", e=2),
+                    in_=acc[:].rearrange("s (e q) -> s q e", e=2),
+                )
+                nc.sync.dma_start(out=rows_out[:, half], in_=result[:, half])

@@ -136,7 +136,6 @@ def tile_instrumentspecificslotmemory_pb_s_kernel(
 
         r_ps = banks.tile([P, D], F32, name="r_ps", tag="a")
         gin_ps = banks.tile([P, D], F32, name="gin_ps", tag="c")
-        ghn_ps = banks.tile([P, D], F32, name="ghn_ps", tag="d")
         bias = keep.tile([P, 2, 3, PACK], F32, name="bias")
         bias_sum = keep.tile([P, 3, PACK], F32, name="bias_sum")
         r = keep.tile([P, D], F32, name="r")
@@ -171,14 +170,30 @@ def tile_instrumentspecificslotmemory_pb_s_kernel(
                 in1=n[:, cols].rearrange("q (t s) -> q t s", t=2), op=ALU.subtract,
             )
 
-        def keep_clock(count):
-            idle_ps = banks.tile([P, P], F32, name="idle_ps", tag="b")
-            for i in range(count):
-                nc.tensor.matmul(idle_ps[:], zeros[:], zeros[:], start=True, stop=True)
+        early_ps = banks.tile([P, P], F32, name="early_ps", tag="d")
 
-        keep_clock(5)
+        def keep_clock(count):
+            for i in range(count):
+                nc.tensor.matmul(early_ps[:], zeros[:], zeros[:], start=True, stop=True)
+
+        def keep_clock_mx(count, tag):
+            idle_ps = banks.tile([P, 2 * P], F32, name="idle_ps", tag=tag)
+            for i in range(count):
+                nc.tensor.matmul_mx(
+                    out=idle_ps[:],
+                    lhsT=q_act[1][:, chunks(AGG)].bitcast(FP8X4),
+                    lhsT_scale=q_act[2][:, chunks(AGG)],
+                    rhs=q_act[1][:].bitcast(FP8X4),
+                    rhs_scale=q_act[2][:],
+                    start=True,
+                    stop=True,
+                )
+
+        keep_clock(3)
         prepare(act_sb, q_act, 0, 2, nc.vector.tensor_copy)
+        keep_clock(1)
         prepare(ih[R], q_ih[R], 0, 2, nc.scalar.copy)
+        keep_clock(1)
         prepare(hh[R], q_hh[R], 0, 2, nc.scalar.copy)
 
         bias_ps = banks.tile([P, P], F32, name="bias_ps", tag="b")
@@ -188,10 +203,14 @@ def tile_instrumentspecificslotmemory_pb_s_kernel(
         )
         nc.vector.tensor_tensor(out=bias_sum[:], in0=bias[:, 0, :, :], in1=bias[:, 1, :, :], op=ALU.add)
 
+        keep_clock(1)
         prepare(ih[N], q_ih[N], 0, 2, nc.scalar.copy)
+        keep_clock(1)
         prepare(hh[N], q_hh[N], 0, 2, nc.scalar.copy)
+        keep_clock(1)
         prepare(ih[R], q_ih[R], 2, 2, nc.scalar.copy)
         r_gate(0)
+        ghn_ps = banks.tile([P, D], F32, name="ghn_ps", tag="d")
         copy_out(transpose(hh[R], 2, 2), q_hh[R], 2, 2, nc.scalar.copy)
         n_products(0)
         quantise(q_hh[R], 2, 2)
@@ -245,6 +264,7 @@ def tile_instrumentspecificslotmemory_pb_s_kernel(
         blended(2, 1, "b")
         blended(3, 1, "a")
         wv_banks.append(transpose(wv_sb, 2, 2))
+        keep_clock_mx(5, "c")
 
         def spread(vector, first, count):
             u, e = first // 2, first % 2
@@ -282,6 +302,7 @@ def tile_instrumentspecificslotmemory_pb_s_kernel(
                 op0=ALU.mult, op1=ALU.add,
             )
             nc.tensor.transpose(m_bank[:, chunks(u)], m_new[:].bitcast(F32)[:, chunks(u)], ident[:])
+        keep_clock_mx(5, "d")
         for tiles in (q_k, q_v):
             for first in (0, 2):
                 quantise(tiles, first, 2)

@@ -67,10 +67,10 @@ def tile_instrumentspecificslotmemory_pb_s_kernel(
                     out=rows[:, u * 2 * D : (u + 1) * 2 * D],
                     in_=w[u * HALF : (u + 1) * HALF, :].rearrange("(p e) k -> p (e k)", e=2),
                 )
-        gain = keep.tile([P, D], BF16, name="gain")
-        shift = keep.tile([P, D], BF16, name="shift")
-        nc.sync.dma_start(out=gain[:], in_=g_mem.partition_broadcast(P))
-        nc.sync.dma_start(out=shift[:], in_=b_mem.partition_broadcast(P))
+        gain_rows = keep.tile([P, 2 * P], BF16, name="gain_rows")
+        nc.gpsimd.memset(gain_rows[:], 0.0)
+        nc.gpsimd.dma_start(out=gain_rows[0:2, :], in_=g_mem.rearrange("(j x) -> j x", x=2 * P))
+        nc.gpsimd.dma_start(out=gain_rows[2:4, :], in_=b_mem.rearrange("(j x) -> j x", x=2 * P))
 
         nc.scalar.dma_start(out=bias_rows[0:6, :], in_=b_ih.rearrange("(j x) -> j x", x=2 * P))
         nc.scalar.dma_start(out=bias_rows[6:12, :], in_=b_hh.rearrange("(j x) -> j x", x=2 * P))
@@ -196,18 +196,18 @@ def tile_instrumentspecificslotmemory_pb_s_kernel(
         keep_clock(1)
         prepare(hh[R], q_hh[R], 0, 2, nc.scalar.copy)
 
+        keep_clock(1)
+        prepare(ih[N], q_ih[N], 0, 2, nc.scalar.copy)
+        keep_clock(1)
+        copy_out(transpose(hh[N], 0, 2), q_hh[N], 0, 2, nc.scalar.copy)
+        keep_clock(1)
         bias_ps = banks.tile([P, P], F32, name="bias_ps", tag="b")
         nc.tensor.transpose(bias_ps[:], bias_rows[:].bitcast(F32), ident[:])
         nc.vector.tensor_copy(
             out=bias[:].rearrange("q a g t -> q (a g t)"), in_=bias_ps[:].bitcast(BF16)[:, 0 : 2 * 3 * PACK]
         )
         nc.vector.tensor_tensor(out=bias_sum[:], in0=bias[:, 0, :, :], in1=bias[:, 1, :, :], op=ALU.add)
-
-        keep_clock(1)
-        prepare(ih[N], q_ih[N], 0, 2, nc.scalar.copy)
-        keep_clock(1)
-        prepare(hh[N], q_hh[N], 0, 2, nc.scalar.copy)
-        keep_clock(1)
+        quantise(q_hh[N], 0, 2)
         prepare(ih[R], q_ih[R], 2, 2, nc.scalar.copy)
         r_gate(0)
         ghn_ps = banks.tile([P, D], F32, name="ghn_ps", tag="d")
@@ -222,6 +222,10 @@ def tile_instrumentspecificslotmemory_pb_s_kernel(
         r_gate(1)
         copy_out(transpose(hh[Z], 0, 2), q_hh[Z], 0, 2, nc.scalar.copy)
         copy_out(transpose(ih[Z], 2, 2), q_ih[Z], 2, 2, nc.scalar.copy)
+        gain_ps = banks.tile([P, P], F32, name="gain_ps", tag="b")
+        nc.tensor.transpose(gain_ps[:], gain_rows[:].bitcast(F32), ident[:])
+        gain_words = keep.tile([P, 4], F32, name="gain_words")
+        nc.vector.tensor_copy(out=gain_words[:], in_=gain_ps[:, 0:4])
         n_products(1)
         quantise(q_hh[Z], 0, 2)
         n_sum(1)
@@ -241,6 +245,9 @@ def tile_instrumentspecificslotmemory_pb_s_kernel(
             out=h[:, chunks(2, 2)].rearrange("q (t s) -> q t s", t=2), in0=m_t[:, 2:4, :],
             in1=n[:, chunks(2, 2)].rearrange("q (t s) -> q t s", t=2), op=ALU.subtract,
         )
+        spread_ps = tpose.tile([P, 4 * P], F32, name="tp")
+        for j in range(4):
+            nc.tensor.transpose(spread_ps[:, chunks(j)], gain_words[:, j : j + 1].to_broadcast([P, P]), ident[:])
         wk_banks.append(transpose(wk_sb, 2, 2))
         wv_banks = [transpose(wv_sb, 0, 2)]
 
@@ -263,7 +270,9 @@ def tile_instrumentspecificslotmemory_pb_s_kernel(
         scaled(3, 1)
         blended(2, 1, "b")
         blended(3, 1, "a")
-        wv_banks.append(transpose(wv_sb, 2, 2))
+        gain = keep.tile([P, D], BF16, name="gain")
+        nc.vector.tensor_copy(out=gain[:].bitcast(F32), in_=spread_ps[:, 0 : 2 * P])
+        shift = spread_ps[:, 2 * P : 4 * P].bitcast(BF16)
         keep_clock_mx(5, "c")
 
         def spread(vector, first, count):
@@ -271,6 +280,7 @@ def tile_instrumentspecificslotmemory_pb_s_kernel(
             return vector[:, u * HALF : (u + 1) * HALF].rearrange("s (q e) -> s e q", e=2)[:, e : e + count, :]
 
         copy_out(wk_banks[0], q_k, 0, 2, nc.scalar.copy)
+        wv_banks.append(transpose(wv_sb, 2, 2))
         stats = keep.tile([P, len(pieces), 6], F32, name="stats")
         for i in range(len(pieces)):
             nc.vector.bn_stats(out=stats[:, i, :], in_=h_ps[i][:])

@@ -145,13 +145,17 @@ def tile_instrumentspecificslotmemory_pb_s_kernel(
         h = keep.tile([P, D], F32, name="h")
         m_t = q_act[0][:, chunks(MOLD * PACK, PACK)].rearrange("q (s t) -> q t s", t=PACK)
 
-        def r_gate(u):
+        def r_products(u):
             gate_product(r_ps, 0, 2 * u, 2, [(q_ih[R], AGG), (q_hh[R], MOLD)])
+
+        def r_gate(u):
             squash(r, r_ps, 0, 2 * u, 2, ACT.Sigmoid, bias_sum[:, R, :])
 
         def n_products(u):
             gate_product(ghn_ps, 0, 2 * u, 2, [(q_hh[N], MOLD)])
             gate_product(gin_ps, 0, 2 * u, 2, [(q_ih[N], AGG)])
+
+        def n_reset(u):
             for t in (2 * u, 2 * u + 1):
                 nc.vector.scalar_tensor_tensor(
                     out=n_pre[:, chunks(t)], in0=ghn_ps[:, chunks(t)], scalar=bias[:, 1, N, t : t + 1], in1=r[:, chunks(t)],
@@ -164,6 +168,8 @@ def tile_instrumentspecificslotmemory_pb_s_kernel(
 
         def n_gate(u):
             squash(n, n_pre, 0, 2 * u, 2, ACT.Tanh, bias[:, 0, N, :])
+
+        def n_distance(u):
             cols = chunks(2 * u, 2)
             nc.vector.tensor_tensor(
                 out=h[:, cols].rearrange("q (t s) -> q t s", t=2), in0=m_t[:, 2 * u : 2 * u + 2, :],
@@ -189,69 +195,17 @@ def tile_instrumentspecificslotmemory_pb_s_kernel(
                     stop=True,
                 )
 
-        keep_clock(3)
-        prepare(act_sb, q_act, 0, 2, nc.vector.tensor_copy)
-        keep_clock(1)
-        prepare(ih[R], q_ih[R], 0, 2, nc.scalar.copy)
-        keep_clock(1)
-        prepare(hh[R], q_hh[R], 0, 2, nc.scalar.copy)
-
-        keep_clock(1)
-        prepare(ih[N], q_ih[N], 0, 2, nc.scalar.copy)
-        keep_clock(1)
-        copy_out(transpose(hh[N], 0, 2), q_hh[N], 0, 2, nc.scalar.copy)
-        keep_clock(1)
-        bias_ps = banks.tile([P, P], F32, name="bias_ps", tag="b")
-        nc.tensor.transpose(bias_ps[:], bias_rows[:].bitcast(F32), ident[:])
-        nc.vector.tensor_copy(
-            out=bias[:].rearrange("q a g t -> q (a g t)"), in_=bias_ps[:].bitcast(BF16)[:, 0 : 2 * 3 * PACK]
-        )
-        nc.vector.tensor_tensor(out=bias_sum[:], in0=bias[:, 0, :, :], in1=bias[:, 1, :, :], op=ALU.add)
-        quantise(q_hh[N], 0, 2)
-        prepare(ih[R], q_ih[R], 2, 2, nc.scalar.copy)
-        r_gate(0)
-        ghn_ps = banks.tile([P, D], F32, name="ghn_ps", tag="d")
-        copy_out(transpose(hh[R], 2, 2), q_hh[R], 2, 2, nc.scalar.copy)
-        n_products(0)
-        quantise(q_hh[R], 2, 2)
-        n_sum(0)
-        prepare(ih[N], q_ih[N], 2, 2, nc.scalar.copy)
-        prepare(hh[N], q_hh[N], 2, 2, nc.scalar.copy)
-        n_gate(0)
-        prepare(ih[Z], q_ih[Z], 0, 2, nc.scalar.copy)
-        r_gate(1)
-        copy_out(transpose(hh[Z], 0, 2), q_hh[Z], 0, 2, nc.scalar.copy)
-        copy_out(transpose(ih[Z], 2, 2), q_ih[Z], 2, 2, nc.scalar.copy)
-        gain_ps = banks.tile([P, P], F32, name="gain_ps", tag="b")
-        nc.tensor.transpose(gain_ps[:], gain_rows[:].bitcast(F32), ident[:])
-        gain_words = keep.tile([P, 4], F32, name="gain_words")
-        nc.vector.tensor_copy(out=gain_words[:], in_=gain_ps[:, 0:4])
-        n_products(1)
-        quantise(q_hh[Z], 0, 2)
-        n_sum(1)
-        quantise(q_ih[Z], 2, 2)
-        prepare(hh[Z], q_hh[Z], 2, 1, nc.scalar.copy)
-        prepare(hh[Z], q_hh[Z], 3, 1, nc.scalar.copy)
+        VEC, SCA = nc.vector.tensor_copy, nc.scalar.copy
         pieces = ((0, 2), (2, 1), (3, 1))
-        squash(n, n_pre, 0, 2, 2, ACT.Tanh, bias[:, 0, N, :])
 
-        wk_banks = [transpose(wk_sb, 0, 2)]
-        for (first, count), tag in zip(pieces, ("b", "a", "c")):
-            z_ps = banks.tile([P, count * P], F32, name="z_ps", tag=tag)
-            gate_product(z_ps, first, first, count, [(q_ih[Z], AGG), (q_hh[Z], MOLD)])
-            squash(z, z_ps, first, first, count, ACT.Sigmoid, bias_sum[:, Z, :])
-        nc.scalar.activation(out=table_warm[:, 1:2], in_=eps[:], func=ACT.Abs_reciprocal_sqrt)
-        nc.vector.tensor_tensor(
-            out=h[:, chunks(2, 2)].rearrange("q (t s) -> q t s", t=2), in0=m_t[:, 2:4, :],
-            in1=n[:, chunks(2, 2)].rearrange("q (t s) -> q t s", t=2), op=ALU.subtract,
-        )
-        spread_ps = tpose.tile([P, 4 * P], F32, name="tp")
-        for j in range(4):
-            nc.tensor.transpose(spread_ps[:, chunks(j)], gain_words[:, j : j + 1].to_broadcast([P, P]), ident[:])
-        wk_banks.append(transpose(wk_sb, 2, 2))
-        wv_banks = [transpose(wv_sb, 0, 2)]
+        def z_products(first, count, tag):
+            bank = banks.tile([P, count * P], F32, name="z_ps", tag=tag)
+            gate_product(bank, first, first, count, [(q_ih[Z], AGG), (q_hh[Z], MOLD)])
+            return bank
 
-        h_ps = []
+        def z_gate(bank, first, count):
+            squash(z, bank, first, first, count, ACT.Sigmoid, bias_sum[:, Z, :])
+
         def scaled(first, count):
             cols = chunks(first, count)
             nc.vector.tensor_tensor(out=h[:, cols], in0=z[:, cols], in1=h[:, cols], op=ALU.mult)
@@ -262,24 +216,100 @@ def tile_instrumentspecificslotmemory_pb_s_kernel(
             bank = banks.tile([P, count * P], F32, name="h_ps", tag=tag)
             for c in range(count):
                 nc.tensor.transpose(bank[:, chunks(c)], h[:, chunks(first + c)], ident[:])
-            h_ps.append(bank)
+            return bank
+
+        keep_clock(3)
+        prepare(act_sb, q_act, 0, 2, VEC)
+        keep_clock(1)
+        prepare(ih[R], q_ih[R], 0, 2, SCA)
+        keep_clock(1)
+        prepare(hh[R], q_hh[R], 0, 2, SCA)
+        keep_clock(1)
+        prepare(ih[N], q_ih[N], 0, 2, SCA)
+        keep_clock(1)
+        copy_out(transpose(hh[N], 0, 2), q_hh[N], 0, 2, SCA)
+        keep_clock(1)
+
+        bias_ps = banks.tile([P, P], F32, name="bias_ps", tag="b")
+        nc.tensor.transpose(bias_ps[:], bias_rows[:].bitcast(F32), ident[:])
+        nc.vector.tensor_copy(
+            out=bias[:].rearrange("q a g t -> q (a g t)"), in_=bias_ps[:].bitcast(BF16)[:, 0 : 2 * 3 * PACK]
+        )
+        nc.vector.tensor_tensor(out=bias_sum[:], in0=bias[:, 0, :, :], in1=bias[:, 1, :, :], op=ALU.add)
+        quantise(q_hh[N], 0, 2)
+        prepare(ih[R], q_ih[R], 2, 2, SCA)
+        r_products(0)
+        r_gate(0)
+        ghn_ps = banks.tile([P, D], F32, name="ghn_ps", tag="d")
+        copy_out(transpose(hh[R], 2, 2), q_hh[R], 2, 2, SCA)
+        copy_out(transpose(ih[N], 2, 2), q_ih[N], 2, 2, SCA)
+        n_products(0)
+        n_reset(0)
+        quantise(q_hh[R], 2, 2)
+        n_sum(0)
+        quantise(q_ih[N], 2, 2)
+        copy_out(transpose(hh[N], 2, 2), q_hh[N], 2, 2, SCA)
+        n_gate(0)
+        copy_out(transpose(ih[Z], 0, 2), q_ih[Z], 0, 2, VEC)
+        r_products(1)
+        r_gate(1)
+        quantise(q_hh[N], 2, 2)
+
+        quantise(q_ih[Z], 0, 2)
+        copy_out(transpose(hh[Z], 0, 2), q_hh[Z], 0, 2, SCA)
+        copy_out(transpose(ih[Z], 2, 2), q_ih[Z], 2, 2, SCA)
+        n_distance(0)
+        gain_ps = banks.tile([P, P], F32, name="gain_ps", tag="b")
+        nc.tensor.transpose(gain_ps[:], gain_rows[:].bitcast(F32), ident[:])
+        gain_words = keep.tile([P, 4], F32, name="gain_words")
+        nc.vector.tensor_copy(out=gain_words[:], in_=gain_ps[:, 0:4])
+
+        last_banks = [transpose(hh[Z], t, 1) for t in (2, 3)]
+        n_products(1)
+        copy_out(last_banks[0], q_hh[Z], 2, 1, SCA)
+        copy_out(last_banks[1], q_hh[Z], 3, 1, SCA)
+        quantise(q_hh[Z], 0, 2)
+        z_a = z_products(0, 2, "b")
+        n_reset(1)
+        quantise(q_ih[Z], 2, 2)
+        z_gate(z_a, 0, 2)
+
+        n_sum(1)
+        quantise(q_hh[Z], 2, 1)
+        quantise(q_hh[Z], 3, 1)
+
+        z_b = z_products(2, 1, "a")
+        z_c = z_products(3, 1, "d")
+        n_gate(1)
+        z_gate(z_b, 2, 1)
+        z_gate(z_c, 3, 1)
+        nc.scalar.activation(out=table_warm[:, 1:2], in_=eps[:], func=ACT.Abs_reciprocal_sqrt)
+        wk_banks = [transpose(wk_sb, 0, 2)]
+        spread_ps = tpose.tile([P, 4 * P], F32, name="tp")
+        for j in range(4):
+            nc.tensor.transpose(spread_ps[:, chunks(j)], gain_words[:, j : j + 1].to_broadcast([P, P]), ident[:])
+
 
         scaled(0, 2)
-        blended(0, 2, "d")
+        n_distance(1)
+        h_ps = [blended(0, 2, "c")]
+
+        wk_banks.append(transpose(wk_sb, 2, 2))
         scaled(2, 1)
         scaled(3, 1)
-        blended(2, 1, "b")
-        blended(3, 1, "a")
+        h_ps.append(blended(2, 1, "b"))
+        h_ps.append(blended(3, 1, "a"))
+        wv_banks = [transpose(wv_sb, 0, 2)]
         gain = keep.tile([P, D], BF16, name="gain")
         nc.vector.tensor_copy(out=gain[:].bitcast(F32), in_=spread_ps[:, 0 : 2 * P])
         shift = spread_ps[:, 2 * P : 4 * P].bitcast(BF16)
-        keep_clock_mx(5, "c")
+        keep_clock_mx(5, "d")
 
         def spread(vector, first, count):
             u, e = first // 2, first % 2
             return vector[:, u * HALF : (u + 1) * HALF].rearrange("s (q e) -> s e q", e=2)[:, e : e + count, :]
 
-        copy_out(wk_banks[0], q_k, 0, 2, nc.scalar.copy)
+        copy_out(wk_banks[0], q_k, 0, 2, SCA)
         wv_banks.append(transpose(wv_sb, 2, 2))
         stats = keep.tile([P, len(pieces), 6], F32, name="stats")
         for i in range(len(pieces)):
@@ -288,9 +318,9 @@ def tile_instrumentspecificslotmemory_pb_s_kernel(
         nc.vector.bn_aggr(out=mean_var[:], in_=stats[:].rearrange("s i x -> s (i x)"))
         rstd = keep.tile([P, 1], F32, name="rstd")
         nc.scalar.activation(out=rstd[:], in_=mean_var[:, 1:2], func=ACT.Abs_reciprocal_sqrt, bias=eps[:, 0:1])
-        copy_out(wk_banks[1], q_k, 2, 2, nc.scalar.copy)
-        copy_out(wv_banks[0], q_v, 0, 2, nc.scalar.copy)
-        copy_out(wv_banks[1], q_v, 2, 2, nc.scalar.copy)
+        copy_out(wk_banks[1], q_k, 2, 2, SCA)
+        copy_out(wv_banks[0], q_v, 0, 2, SCA)
+        copy_out(wv_banks[1], q_v, 2, 2, SCA)
         centred = keep.tile([P, D], F32, name="centred")
         for i, (first, count) in enumerate(pieces):
             nc.vector.scalar_tensor_tensor(
@@ -301,7 +331,7 @@ def tile_instrumentspecificslotmemory_pb_s_kernel(
                 op0=ALU.subtract, op1=ALU.mult,
             )
         m_new = keep.tile([P, D], BF16, name="m_new")
-        m_bank = banks.tile([P, 2 * P], F32, name="m_bank", tag="c")
+        m_bank = banks.tile([P, 2 * P], F32, name="m_bank", tag="b")
         for u in range(2):
             half = slice(u * HALF, (u + 1) * HALF)
             nc.vector.scalar_tensor_tensor(
@@ -316,7 +346,7 @@ def tile_instrumentspecificslotmemory_pb_s_kernel(
         for tiles in (q_k, q_v):
             for first in (0, 2):
                 quantise(tiles, first, 2)
-        copy_out(m_bank, q_m, 0, 1, nc.scalar.copy)
+        copy_out(m_bank, q_m, 0, 1, SCA)
         quantise(q_m, 0, 1)
 
         for name, (grouped, codes, scales), out in (("kt", q_k, out_0), ("v", q_v, out_1)):

@@ -39,12 +39,12 @@ def tile_instrumentspecificslotmemory_pb_s_kernel(
 
         ident = keep.tile([P, P], F32, name="ident")
         make_identity(nc, ident[:])
+        zeros = keep.tile([P, P], F32, name="zeros")
+        nc.vector.memset(zeros[:], 0.0)
         bias_rows = keep.tile([P, 2 * P], BF16, name="bias_rows")
         nc.vector.memset(bias_rows[:], 0.0)
         eps = keep.tile([P, 1], F32, name="eps")
         nc.vector.memset(eps[:], EPS)
-        zeros = keep.tile([P, P], F32, name="zeros")
-        nc.vector.memset(zeros[:], 0.0)
 
         act_sb = keep.tile([P, 2 * D], BF16, name="act_sb")
         nc.sync.dma_start(out=act_sb[:, 0:D], in_=agg.rearrange("b s d -> (b s) d"))
@@ -218,7 +218,7 @@ def tile_instrumentspecificslotmemory_pb_s_kernel(
                 nc.tensor.transpose(bank[:, chunks(c)], h[:, chunks(first + c)], ident[:])
             return bank
 
-        keep_clock(3)
+        keep_clock(4)
         prepare(act_sb, q_act, 0, 2, VEC)
         keep_clock(1)
         prepare(ih[R], q_ih[R], 0, 2, SCA)
@@ -343,11 +343,12 @@ def tile_instrumentspecificslotmemory_pb_s_kernel(
             )
             nc.tensor.transpose(m_bank[:, chunks(u)], m_new[:].bitcast(F32)[:, chunks(u)], ident[:])
         keep_clock_mx(5, "d")
-        for tiles in (q_k, q_v):
-            for first in (0, 2):
-                quantise(tiles, first, 2)
-        copy_out(m_bank, q_m, 0, 1, SCA)
+        for first in (0, 2):
+            quantise(q_k, first, 2)
+        copy_out(m_bank, q_m, 0, 1, VEC)
         quantise(q_m, 0, 1)
+        for first in (0, 2):
+            quantise(q_v, first, 2)
 
         for name, (grouped, codes, scales), out in (("kt", q_k, out_0), ("v", q_v, out_1)):
             result = keep.tile([P, D], F32, name=name)

from contextlib import ExitStack

import concourse.mybir as mybir
from concourse.masks import make_identity

BF16 = mybir.dt.bfloat16
F32 = mybir.dt.float32
U32 = mybir.dt.uint32
U8 = mybir.dt.uint8
FP8X4 = mybir.dt.float8_e4m3fn_x4
ACT = mybir.ActivationFunctionType
ALU = mybir.AluOpType

P = 128
D = 512
PACK = 4
HALF = D // 2
WORDS = D // 2
EPS = 1e-5
R, Z, N = 0, 1, 2
AGG, MOLD = 0, 1

FLOPS = 2 * P * D * (2 * 3 * D + 2 * D)


def chunks(first, count=1):
    return slice(first * P, (first + count) * P)


def tile_instrumentspecificslotmemory_pb_s_kernel(
    tc, agg, M_old, W_ih, W_hh, b_ih, b_hh, g_mem, b_mem, Wk, Wv, out_0, out_1
):
    nc = tc.nc
    with ExitStack() as ctx:
        ctx.enter_context(tc.manual_schedule())
        keep = ctx.enter_context(tc.tile_pool(name="keep", bufs=1))
        tpose = ctx.enter_context(tc.psum_pool(name="tpose", bufs=4))
        banks = ctx.enter_context(tc.psum_pool(name="banks", bufs=1))

        ident = keep.tile([P, P], F32, name="ident")
        make_identity(nc, ident[:])
        zeros = keep.tile([P, P], F32, name="zeros")
        nc.vector.memset(zeros[:], 0.0)
        bias_rows = keep.tile([P, 2 * P], BF16, name="bias_rows")
        nc.vector.memset(bias_rows[:], 0.0)
        eps = keep.tile([P, 1], F32, name="eps")
        nc.vector.memset(eps[:], EPS)

        act_sb = keep.tile([P, 2 * D], BF16, name="act_sb")
        nc.sync.dma_start(out=act_sb[:, 0:D], in_=agg.rearrange("b s d -> (b s) d"))
        nc.sync.dma_start(out=act_sb[:, D : 2 * D], in_=M_old.rearrange("b s d -> (b s) d"))

        ih = [keep.tile([P, PACK * D], BF16, name="ih%d" % gate) for gate in range(3)]
        hh = [keep.tile([P, PACK * D], BF16, name="hh%d" % gate) for gate in range(3)]
        for gate, u in ((R, 0), (N, 0), (R, 1), (N, 1), (Z, 0), (Z, 1)):
            for rows, w in ((ih[gate], W_ih), (hh[gate], W_hh)):
                first = gate * D + u * HALF
                nc.sync.dma_start(
                    out=rows[:, u * 2 * D : (u + 1) * 2 * D],
                    in_=w[first : first + HALF, :].rearrange("(p e) k -> p (e k)", e=2),
                )
        wk_sb = keep.tile([P, PACK * D], BF16, name="wk_sb")
        wv_sb = keep.tile([P, PACK * D], BF16, name="wv_sb")
        for rows, w in ((wk_sb, Wk), (wv_sb, Wv)):
            for u in range(2):
                nc.sync.dma_start(
                    out=rows[:, u * 2 * D : (u + 1) * 2 * D],
                    in_=w[u * HALF : (u + 1) * HALF, :].rearrange("(p e) k -> p (e k)", e=2),
                )
        gain_rows = keep.tile([P, 2 * P], BF16, name="gain_rows")
        nc.gpsimd.memset(gain_rows[:], 0.0)
        nc.gpsimd.dma_start(out=gain_rows[0:2, :], in_=g_mem.rearrange("(j x) -> j x", x=2 * P))
        nc.gpsimd.dma_start(out=gain_rows[2:4, :], in_=b_mem.rearrange("(j x) -> j x", x=2 * P))

        nc.scalar.dma_start(out=bias_rows[0:6, :], in_=b_ih.rearrange("(j x) -> j x", x=2 * P))
        nc.scalar.dma_start(out=bias_rows[6:12, :], in_=b_hh.rearrange("(j x) -> j x", x=2 * P))
        table_warm = keep.tile([P, 2], F32, name="table_warm")
        nc.scalar.activation(out=table_warm[:, 0:1], in_=eps[:], func=ACT.Sigmoid)

        def transpose(rows, first, count):
            words = rows[:].bitcast(F32)
            bank = tpose.tile([P, count * 2 * P], F32, name="tp")
            for c in range(count):
                for u in range(2):
                    start = (first + c) * WORDS + u * P
                    nc.tensor.transpose(bank[:, chunks(2 * c + u)], words[:, start : start + P], ident[:])
            return bank

        def copy_out(bank, tiles, first, count, copy):
            grouped, codes, scales = tiles
            copy(
                out=grouped[:, chunks(first * PACK, count * PACK)].bitcast(F32).rearrange("q (c r u) -> q c r u", c=count, u=2),
                in_=bank[:].rearrange("q (c u r) -> q c r u", c=count, u=2),
            )

        def quantise(tiles, first, count):
            grouped, codes, scales = tiles
            nc.vector.quantize_mx(
                out=codes[:, chunks(first, count)].bitcast(FP8X4),
                scales=scales[:, chunks(first, count)],
                in_=grouped[:, chunks(first * PACK, count * PACK)],
            )

        def prepare(rows, tiles, first, count, copy):
            copy_out(transpose(rows, first, count), tiles, first, count, copy)
            quantise(tiles, first, count)

        def operand(name, count):
            grouped = keep.tile([P, count * P * PACK], BF16, name=name + "_grouped", align_bytes=64)
            codes = keep.tile([P, count * P], U32, name=name + "_codes", align_bytes=64)
            scales = keep.tile([P, count * P], U8, name=name + "_scales", align_bytes=64)
            return grouped, codes, scales

        q_act = operand("act", 2)
        q_ih = [operand("q_ih%d" % gate, PACK) for gate in range(3)]
        q_hh = [operand("q_hh%d" % gate, PACK) for gate in range(3)]
        q_k, q_v = operand("wk", PACK), operand("wv", PACK)
        q_m = operand("m_new", 1)

        def gate_product(bank, base, first, count, terms):
            for t in range(first, first + count):
                for i, ((grouped, codes, scales), a) in enumerate(terms):
                    nc.tensor.matmul_mx(
                        out=bank[:, chunks(t - base)],
                        lhsT=codes[:, chunks(t)].bitcast(FP8X4),
                        lhsT_scale=scales[:, chunks(t)],
                        rhs=q_act[1][:, chunks(a)].bitcast(FP8X4),
                        rhs_scale=q_act[2][:, chunks(a)],
                        start=(i == 0),
                        stop=(i == len(terms) - 1),
                    )

        def squash(out, pre, base, first, count, func, bias):
            for t in range(first, first + count):
                nc.scalar.activation(out=out[:, chunks(t)], in_=pre[:, chunks(t - base)], func=func, bias=bias[:, t : t + 1])

        r_ps = banks.tile([P, D], F32, name="r_ps", tag="a")
        gin_ps = banks.tile([P, D], F32, name="gin_ps", tag="c")
        bias = keep.tile([P, 2, 3, PACK], F32, name="bias")
        bias_sum = keep.tile([P, 3, PACK], F32, name="bias_sum")
        r = keep.tile([P, D], F32, name="r")
        n_pre = keep.tile([P, D], F32, name="n_pre")
        n = keep.tile([P, D], F32, name="n")
        z = keep.tile([P, D], F32, name="z")
        h = keep.tile([P, D], F32, name="h")
        m_t = q_act[0][:, chunks(MOLD * PACK, PACK)].rearrange("q (s t) -> q t s", t=PACK)

        def r_products(u):
            gate_product(r_ps, 0, 2 * u, 2, [(q_ih[R], AGG), (q_hh[R], MOLD)])

        def r_gate(u):
            squash(r, r_ps, 0, 2 * u, 2, ACT.Sigmoid, bias_sum[:, R, :])

        def n_products(u):
            gate_product(ghn_ps, 0, 2 * u, 2, [(q_hh[N], MOLD)])
            gate_product(gin_ps, 0, 2 * u, 2, [(q_ih[N], AGG)])

        def n_reset(u):
            for t in (2 * u, 2 * u + 1):
                nc.vector.scalar_tensor_tensor(
                    out=n_pre[:, chunks(t)], in0=ghn_ps[:, chunks(t)], scalar=bias[:, 1, N, t : t + 1], in1=r[:, chunks(t)],
                    op0=ALU.add, op1=ALU.mult,
                )

        def n_sum(u):
            cols = chunks(2 * u, 2)
            nc.vector.tensor_tensor(out=n_pre[:, cols], in0=gin_ps[:, cols], in1=n_pre[:, cols], op=ALU.add)

        def n_gate(u):
            squash(n, n_pre, 0, 2 * u, 2, ACT.Tanh, bias[:, 0, N, :])

        def n_distance(u):
            cols = chunks(2 * u, 2)
            nc.vector.tensor_tensor(
                out=h[:, cols].rearrange("q (t s) -> q t s", t=2), in0=m_t[:, 2 * u : 2 * u + 2, :],
                in1=n[:, cols].rearrange("q (t s) -> q t s", t=2), op=ALU.subtract,
            )

        early_ps = banks.tile([P, P], F32, name="early_ps", tag="d")

        def keep_clock(count):
            for i in range(count):
                nc.tensor.matmul(early_ps[:], zeros[:], zeros[:], start=True, stop=True)

        def keep_clock_mx(count, tag):
            idle_ps = banks.tile([P, 2 * P], F32, name="idle_ps", tag=tag)
            for i in range(count):
                nc.tensor.matmul_mx(
                    out=idle_ps[:],
                    lhsT=q_act[1][:, chunks(AGG)].bitcast(FP8X4),
                    lhsT_scale=q_act[2][:, chunks(AGG)],
                    rhs=q_act[1][:].bitcast(FP8X4),
                    rhs_scale=q_act[2][:],
                    start=True,
                    stop=True,
                )

        VEC, SCA = nc.vector.tensor_copy, nc.scalar.copy
        pieces = ((0, 2), (2, 1), (3, 1))

        def z_products(first, count, tag):
            bank = banks.tile([P, count * P], F32, name="z_ps", tag=tag)
            gate_product(bank, first, first, count, [(q_ih[Z], AGG), (q_hh[Z], MOLD)])
            return bank

        def z_gate(bank, first, count):
            squash(z, bank, first, first, count, ACT.Sigmoid, bias_sum[:, Z, :])

        def scaled(first, count):
            cols = chunks(first, count)
            nc.vector.tensor_tensor(out=h[:, cols], in0=z[:, cols], in1=h[:, cols], op=ALU.mult)

        def blended(first, count, tag):
            cols = chunks(first, count)
            nc.vector.tensor_tensor(out=h[:, cols], in0=h[:, cols], in1=n[:, cols], op=ALU.add)
            bank = banks.tile([P, count * P], F32, name="h_ps", tag=tag)
            for c in range(count):
                nc.tensor.transpose(bank[:, chunks(c)], h[:, chunks(first + c)], ident[:])
            return bank

        keep_clock(4)
        prepare(act_sb, q_act, 0, 2, VEC)
        keep_clock(1)
        prepare(ih[R], q_ih[R], 0, 2, SCA)
        keep_clock(1)
        prepare(hh[R], q_hh[R], 0, 2, SCA)
        keep_clock(1)
        prepare(ih[N], q_ih[N], 0, 2, SCA)
        keep_clock(1)
        copy_out(transpose(hh[N], 0, 2), q_hh[N], 0, 2, SCA)
        keep_clock(1)

        bias_ps = banks.tile([P, P], F32, name="bias_ps", tag="b")
        nc.tensor.transpose(bias_ps[:], bias_rows[:].bitcast(F32), ident[:])
        nc.vector.tensor_copy(
            out=bias[:].rearrange("q a g t -> q (a g t)"), in_=bias_ps[:].bitcast(BF16)[:, 0 : 2 * 3 * PACK]
        )
        nc.vector.tensor_tensor(out=bias_sum[:], in0=bias[:, 0, :, :], in1=bias[:, 1, :, :], op=ALU.add)
        quantise(q_hh[N], 0, 2)
        prepare(ih[R], q_ih[R], 2, 2, SCA)
        r_products(0)
        r_gate(0)
        ghn_ps = banks.tile([P, D], F32, name="ghn_ps", tag="d")
        copy_out(transpose(hh[R], 2, 2), q_hh[R], 2, 2, SCA)
        copy_out(transpose(ih[N], 2, 2), q_ih[N], 2, 2, SCA)
        n_products(0)
        n_reset(0)
        quantise(q_hh[R], 2, 2)
        n_sum(0)
        quantise(q_ih[N], 2, 2)
        copy_out(transpose(hh[N], 2, 2), q_hh[N], 2, 2, SCA)
        n_gate(0)
        copy_out(transpose(ih[Z], 0, 2), q_ih[Z], 0, 2, VEC)
        r_products(1)
        r_gate(1)
        quantise(q_hh[N], 2, 2)

        quantise(q_ih[Z], 0, 2)
        copy_out(transpose(hh[Z], 0, 2), q_hh[Z], 0, 2, SCA)
        copy_out(transpose(ih[Z], 2, 2), q_ih[Z], 2, 2, SCA)
        n_distance(0)
        gain_ps = banks.tile([P, P], F32, name="gain_ps", tag="b")
        nc.tensor.transpose(gain_ps[:], gain_rows[:].bitcast(F32), ident[:])
        gain_words = keep.tile([P, 4], F32, name="gain_words")
        nc.vector.tensor_copy(out=gain_words[:], in_=gain_ps[:, 0:4])

        last_banks = [transpose(hh[Z], t, 1) for t in (2, 3)]
        n_products(1)
        copy_out(last_banks[0], q_hh[Z], 2, 1, SCA)
        copy_out(last_banks[1], q_hh[Z], 3, 1, SCA)
        quantise(q_hh[Z], 0, 2)
        z_a = z_products(0, 2, "b")
        n_reset(1)
        quantise(q_ih[Z], 2, 2)
        z_gate(z_a, 0, 2)

        n_sum(1)
        quantise(q_hh[Z], 2, 1)
        quantise(q_hh[Z], 3, 1)

        z_b = z_products(2, 1, "a")
        z_c = z_products(3, 1, "d")
        n_gate(1)
        z_gate(z_b, 2, 1)
        z_gate(z_c, 3, 1)
        nc.scalar.activation(out=table_warm[:, 1:2], in_=eps[:], func=ACT.Abs_reciprocal_sqrt)
        wk_banks = [transpose(wk_sb, 0, 2)]
        spread_ps = tpose.tile([P, 4 * P], F32, name="tp")
        for j in range(4):
            nc.tensor.transpose(spread_ps[:, chunks(j)], gain_words[:, j : j + 1].to_broadcast([P, P]), ident[:])


        scaled(0, 2)
        n_distance(1)
        h_ps = [blended(0, 2, "c")]

        wk_banks.append(transpose(wk_sb, 2, 2))
        scaled(2, 1)
        scaled(3, 1)
        h_ps.append(blended(2, 1, "b"))
        h_ps.append(blended(3, 1, "a"))
        wv_banks = [transpose(wv_sb, 0, 2)]
        gain = keep.tile([P, D], BF16, name="gain")
        nc.vector.tensor_copy(out=gain[:].bitcast(F32), in_=spread_ps[:, 0 : 2 * P])
        shift = spread_ps[:, 2 * P : 4 * P].bitcast(BF16)
        keep_clock_mx(5, "d")

        def spread(vector, first, count):
            u, e = first // 2, first % 2
            return vector[:, u * HALF : (u + 1) * HALF].rearrange("s (q e) -> s e q", e=2)[:, e : e + count, :]

        copy_out(wk_banks[0], q_k, 0, 2, SCA)
        wv_banks.append(transpose(wv_sb, 2, 2))
        stats = keep.tile([P, len(pieces), 6], F32, name="stats")
        for i in range(len(pieces)):
            nc.vector.bn_stats(out=stats[:, i, :], in_=h_ps[i][:])
        mean_var = keep.tile([P, 2], F32, name="mean_var")
        nc.vector.bn_aggr(out=mean_var[:], in_=stats[:].rearrange("s i x -> s (i x)"))
        rstd = keep.tile([P, 1], F32, name="rstd")
        nc.scalar.activation(out=rstd[:], in_=mean_var[:, 1:2], func=ACT.Abs_reciprocal_sqrt, bias=eps[:, 0:1])
        copy_out(wk_banks[1], q_k, 2, 2, SCA)
        copy_out(wv_banks[0], q_v, 0, 2, SCA)
        copy_out(wv_banks[1], q_v, 2, 2, SCA)
        centred = keep.tile([P, D], F32, name="centred")
        for i, (first, count) in enumerate(pieces):
            nc.vector.scalar_tensor_tensor(
                out=centred[:, chunks(first, count)].rearrange("s (t q) -> s t q", t=count),
                in0=h_ps[i][:].rearrange("s (t q) -> s t q", t=count),
                scalar=mean_var[:, 0:1],
                in1=spread(gain, first, count),
                op0=ALU.subtract, op1=ALU.mult,
            )
        m_new = keep.tile([P, D], BF16, name="m_new")
        m_bank = banks.tile([P, 2 * P], F32, name="m_bank", tag="b")
        for u in range(2):
            half = slice(u * HALF, (u + 1) * HALF)
            nc.vector.scalar_tensor_tensor(
                out=m_new[:, half].rearrange("s (q e) -> s q e", e=2),
                in0=centred[:, chunks(2 * u, 2)].rearrange("s (e q) -> s q e", e=2),
                scalar=rstd[:, 0:1],
                in1=shift[:, half].rearrange("s (q e) -> s q e", e=2),
                op0=ALU.mult, op1=ALU.add,
            )
            nc.tensor.transpose(m_bank[:, chunks(u)], m_new[:].bitcast(F32)[:, chunks(u)], ident[:])
        keep_clock_mx(5, "d")
        for first in (0, 2):
            quantise(q_k, first, 2)
        copy_out(m_bank, q_m, 0, 1, VEC)
        quantise(q_m, 0, 1)
        for first in (0, 2):
            quantise(q_v, first, 2)

        for name, (grouped, codes, scales), out in (("kt", q_k, out_0), ("v", q_v, out_1)):
            result = keep.tile([P, D], F32, name=name)
            rows_out = out.rearrange("b s d -> (b s) d")
            for u, copy in ((0, nc.scalar.copy), (1, nc.vector.tensor_copy)):
                half = slice(u * HALF, (u + 1) * HALF)
                acc = tpose.tile([P, HALF], F32, name="tp")
                nc.tensor.matmul_mx(
                    out=acc[:],
                    lhsT=q_m[1][:].bitcast(FP8X4),
                    lhsT_scale=q_m[2][:],
                    rhs=codes[:, chunks(2 * u, 2)].bitcast(FP8X4),
                    rhs_scale=scales[:, chunks(2 * u, 2)],
                    start=True,
                    stop=True,
                )
                copy(
                    out=result[:, half].rearrange("s (q e) -> s q e", e=2),
                    in_=acc[:].rearrange("s (e q) -> s q e", e=2),
                )
                nc.sync.dma_start(out=rows_out[:, half], in_=result[:, half])
